import numpy as np
import ml_dtypes


def mxq(x, axis, fmt="e4m3"):
    dtype, down = {"e4m3": (ml_dtypes.float8_e4m3fn, 7), "e5m2": (ml_dtypes.float8_e5m2, 14)}[fmt]
    v = np.moveaxis(np.asarray(x, np.float32).astype(ml_dtypes.bfloat16).astype(np.float64), axis, -1)
    blocks = v.reshape(v.shape[:-1] + (-1, 32))
    amax = np.abs(blocks).max(-1, keepdims=True)
    byte = np.maximum(np.where(amax > 0, np.frexp(amax)[1] - 1 + 127, 0) - down, 1)
    scale = np.exp2(byte - 127.0)
    codes = (blocks / scale).astype(np.float32).astype(dtype).astype(np.float64)
    return np.moveaxis((codes * scale).reshape(v.shape), -1, axis)


WIDE = False


def mx_kscale(k):
    if not WIDE:
        return np.ones(k)
    levels = np.array([10, -10, 5, -5, 0])
    a = np.random.permutation(np.resize(levels, k // 512 * 4)).reshape(k // 512, 4)
    idx = np.arange(k)
    return np.exp2(a[idx // 512, idx % 128 // 32])


BF16 = ml_dtypes.bfloat16


def bf(x):
    return np.asarray(x, np.float32).astype(BF16)


def f64(x):
    return np.asarray(x).astype(np.float64)


E2M1 = np.array([0.0, 0.5, 1.0, 1.5, 2.0, 3.0, 4.0, 6.0, -0.0, -0.5, -1.0, -1.5, -2.0, -3.0, -4.0, -6.0])


def pack_weight(w, fmt):
    k, n = w.shape
    w = f64(bf(w)).reshape(k // 32, 32, n)
    amax = np.abs(w).max(1)
    if fmt == "e4m3":
        byte = np.frexp(amax)[1] - 1 + 127 - 7
    else:
        mant, ex = np.frexp(amax / 6.0)
        byte = np.where(mant > 0.5, ex, ex - 1) + 127
    byte = np.clip(np.where(amax > 0, byte, 1), 1, 254)
    scaled = (w * np.exp2(127.0 - byte)[:, None, :]).reshape(k, n).astype(np.float32)
    by_word = np.ascontiguousarray(scaled.reshape(k // 512, 128, 4, n).transpose(0, 1, 3, 2))
    if fmt == "e4m3":
        words = by_word.astype(ml_dtypes.float8_e4m3fn).view(np.uint8)
    else:
        c = by_word.astype(ml_dtypes.float4_e2m1fn).view(np.uint8) & 0xF
        words = c[..., 0::2] | (c[..., 1::2] << 4)
    return np.ascontiguousarray(words), np.ascontiguousarray(byte.astype(np.uint8).reshape(k // 512, 16, n))


def unpack_weight(words, scales, fmt):
    g, p, n, _ = words.shape
    if fmt == "e4m3":
        vals = np.ascontiguousarray(words).view(ml_dtypes.float8_e4m3fn).astype(np.float64)
    else:
        nib = np.empty((g, p, n, 4), np.uint8)
        nib[..., 0::2] = words & 0xF
        nib[..., 1::2] = words >> 4
        vals = E2M1[nib]
    vals = vals * np.repeat(np.exp2(scales.astype(np.float64) - 127.0), 8, axis=1)[..., None]
    return vals.transpose(0, 1, 3, 2).reshape(g * 512, n)


B, S, H, NH, HD, W = 2, 64, 8192, 8, 64, 4
D = NH * HD
EPS = 1e-5
FMT = "e4m3"


def layernorm(x, scale, bias):
    mu = x.mean(-1, keepdims=True)
    var = np.square(x - mu).mean(-1, keepdims=True)
    return (x - mu) / np.sqrt(var + EPS) * scale + bias


def rope(x, pos):
    half = HD // 2
    freq = 1.0 / (10000.0 ** (np.arange(half) / half))
    ang = pos[:, None] * freq[None, :]
    cos = np.cos(ang)[None, :, None, :]
    sin = np.sin(ang)[None, :, None, :]
    x1, x2 = x[..., :half], x[..., half:]
    return np.concatenate([x1 * cos - x2 * sin, x1 * sin + x2 * cos], axis=-1)


def setup_inputs():
    s = mx_kscale(H)
    hidden_states = bf(np.random.standard_normal((B, S, H)) + 0.5 * np.random.standard_normal((B, S, 1)))
    cache_states = bf(np.random.standard_normal((W, B, S, H)) * s)
    ln_scale = bf((1.0 + 0.1 * np.random.standard_normal(H)) * s)
    ln_bias = bf(0.1 * np.random.standard_normal(H) * s)
    Wq_words, Wq_scales = pack_weight(np.random.standard_normal((H, D)) * 1.4 / np.sqrt(H) / s[:, None], FMT)
    Wk_words, Wk_scales = pack_weight(np.random.standard_normal((H, D)) * 1.4 / np.sqrt(H) / s[:, None], FMT)
    Wv_words, Wv_scales = pack_weight(np.random.standard_normal((H, D)) * 2.0 / np.sqrt(H) / s[:, None], FMT)
    return {"hidden_states": hidden_states,
            "cache_states": cache_states,
            "ln_scale": ln_scale,
            "ln_bias": ln_bias,
            "Wq_words": Wq_words, "Wq_scales": Wq_scales,
            "Wk_words": Wk_words, "Wk_scales": Wk_scales,
            "Wv_words": Wv_words, "Wv_scales": Wv_scales}


def reference(hidden_states, cache_states, ln_scale, ln_bias, Wq_words, Wq_scales, Wk_words, Wk_scales, Wv_words, Wv_scales):
    normed = layernorm(f64(hidden_states), f64(ln_scale), f64(ln_bias))
    prev_flat = np.transpose(f64(cache_states), (1, 0, 2, 3)).reshape(B, W * S, H)
    nq = mxq(normed, 2, "e4m3")
    pq = mxq(prev_flat, 2, "e4m3")
    wkq = unpack_weight(Wk_words, Wk_scales, FMT)
    wvq = unpack_weight(Wv_words, Wv_scales, FMT)
    q = (nq @ unpack_weight(Wq_words, Wq_scales, FMT)).reshape(B, S, NH, HD)
    k = np.concatenate([(pq @ wkq), (nq @ wkq)], axis=1).reshape(B, (W + 1) * S, NH, HD)
    v = np.concatenate([(pq @ wvq), (nq @ wvq)], axis=1).reshape(B, (W + 1) * S, NH, HD)
    q_rot = rope(q, np.arange(S))
    k_rot = rope(k, np.tile(np.arange(S), W + 1))
    return q_rot, k_rot, v

@@ -1,0 +1,366 @@
+import math
+from contextlib import ExitStack
+
+import concourse.mybir as mybir
+from concourse.masks import make_identity
+
+F32 = mybir.dt.float32
+BF16 = mybir.dt.bfloat16
+I32 = mybir.dt.int32
+U32 = mybir.dt.uint32
+U8 = mybir.dt.uint8
+FP8X4 = mybir.dt.float8_e4m3fn_x4
+ALU = mybir.AluOpType
+ACT = mybir.ActivationFunctionType
+
+P = 128
+PACK = 4
+GROUP = P * PACK
+FEATURES = 8192
+GROUPS = FEATURES // GROUP
+CHUNK_GROUPS = 4
+CHUNKS = GROUPS // CHUNK_GROUPS
+CHUNK = CHUNK_GROUPS * GROUP
+COLS = 512
+HEADS = 8
+HALF = 32
+SEQ = 64
+BATCH = 2
+LAYERS = 4
+HIDDEN = LAYERS
+EPS = 1e-5
+QUADRANTS = 4
+PAIR = 2
+STEPS = CHUNKS * LAYERS // PAIR
+RING = 8
+AHEAD = RING // PAIR
+STATS_STEP = 3
+
+FLOPS = 2 * FEATURES * COLS * (P + 2 * (LAYERS + 1) * P)
+
+
+def tile_mlablock_pa_k_kernel(
+    tc,
+    hidden_states,
+    cache_states,
+    ln_scale,
+    ln_bias,
+    Wq_words,
+    Wq_scales,
+    Wk_words,
+    Wk_scales,
+    Wv_words,
+    Wv_scales,
+    out_0,
+    out_1,
+    out_2,
+):
+    nc = tc.nc
+    with ExitStack() as ctx:
+        const = ctx.enter_context(tc.tile_pool(name="const", bufs=1))
+        keep = ctx.enter_context(tc.tile_pool(name="keep", bufs=1))
+        ring = ctx.enter_context(tc.tile_pool(name="ring", bufs=RING))
+        stage = ctx.enter_context(tc.tile_pool(name="stage", bufs=2))
+        banks = ctx.enter_context(tc.psum_pool(name="banks", bufs=4))
+        ctx.enter_context(tc.manual_schedule())
+
+        cache_rows = cache_states.rearrange("w b s k -> w (b s) k")
+        hidden_rows = hidden_states.rearrange("b s k -> (b s) k")
+        q_rows = out_0.rearrange("b s h d -> (b s) (h d)")
+        k_rows = out_1.rearrange("b l h d -> b l (h d)")
+        v_rows = out_2.rearrange("b l h d -> b l (h d)")
+        dram_words = {"q": Wq_words, "k": Wk_words, "v": Wv_words}
+        dram_scales = {"q": Wq_scales, "k": Wk_scales, "v": Wv_scales}
+
+        plane_tiles = {}
+        for w in ("k", "v", "q"):
+            plane_tiles[w] = keep.tile([P, CHUNKS, COLS], U8, align_bytes=64, name="planes_" + w)
+            nc.vector.memset(plane_tiles[w][:].bitcast(I32), 0)
+        gain_bias_rows = const.tile([P, GROUP], BF16)
+        nc.vector.memset(gain_bias_rows[:], 0.0)
+
+        codes = [keep.tile([P, GROUPS, P], U32, align_bytes=64, name="codes%d" % i) for i in range(LAYERS + 1)]
+        code_planes = [keep.tile([P, GROUPS, P], U8, align_bytes=64, name="cplanes%d" % i) for i in range(LAYERS + 1)]
+
+        weight_words = {"q": [], "k": [], "v": []}
+        weight_planes = {"q": [], "k": [], "v": []}
+
+        identity = const.tile([P, P], F32)
+        make_identity(nc, identity[:])
+
+        def load_scales(w, c):
+            for quadrant in range(QUADRANTS):
+                first = 32 * quadrant
+                nc.sync.dma_start(
+                    out=plane_tiles[w][first : first + 16, c, :].bitcast(I32),
+                    in_=dram_scales[w][
+                        CHUNK_GROUPS * c : CHUNK_GROUPS * (c + 1), 4 * quadrant : 4 * quadrant + 4, :
+                    ].bitcast(I32),
+                )
+            for i in range(CHUNK_GROUPS):
+                weight_planes[w].append(plane_tiles[w][4 * i : P, c, :])
+
+        def load_words(w, tile_, first_group, groups):
+            source = dram_words[w][first_group : first_group + groups].rearrange("g p n t -> p g (n t)")
+            nc.sync.dma_start(out=tile_[:].bitcast(I32), in_=source.bitcast(I32))
+            for i in range(groups):
+                weight_words[w].append(tile_[:, i, :])
+
+        def load_resident_chunk(w, c):
+            load_scales(w, c)
+            chunk_words = keep.tile([P, CHUNK_GROUPS, COLS], U32, align_bytes=64, name="words_%s%d" % (w, c))
+            load_words(w, chunk_words, CHUNK_GROUPS * c, CHUNK_GROUPS)
+
+        cached = {}
+
+        def load_step(step):
+            c, pair = divmod(step, LAYERS // PAIR)
+            if pair == 0:
+                load_scales("k", c)
+            for i in range(PAIR * pair, PAIR * (pair + 1)):
+                cached[(i, c)] = ring.tile([P, CHUNK], BF16, align_bytes=64, tag="ring", name="cached")
+                nc.sync.dma_start(out=cached[(i, c)][:], in_=cache_rows[i, :, CHUNK * c : CHUNK * (c + 1)])
+            if pair == 0:
+                chunk_words = keep.tile([P, CHUNK_GROUPS, COLS], U32, align_bytes=64, name="words_k%d" % c)
+                load_words("k", chunk_words, CHUNK_GROUPS * c, CHUNK_GROUPS)
+
+        for step in range(AHEAD):
+            load_step(step)
+        hidden_raw = keep.tile([P, FEATURES], BF16)
+        nc.sync.dma_start(out=hidden_raw[:], in_=hidden_rows)
+        nc.sync.dma_start(out=gain_bias_rows[0:GROUPS, :], in_=ln_scale.rearrange("(g k) -> g k", k=GROUP))
+        nc.sync.dma_start(out=gain_bias_rows[GROUPS : 2 * GROUPS, :], in_=ln_bias.rearrange("(g k) -> g k", k=GROUP))
+
+        partition_index = const.tile([P, 1], I32)
+        nc.gpsimd.iota(partition_index[:], pattern=[[0, 1]], base=0, channel_multiplier=1)
+        pos_int = const.tile([P, 1], I32)
+        nc.vector.tensor_single_scalar(out=pos_int[:], in_=partition_index[:], scalar=SEQ - 1, op=ALU.bitwise_and)
+        pos = const.tile([P, 1], F32)
+        nc.vector.tensor_copy(out=pos[:], in_=pos_int[:])
+        freq = const.tile([P, HALF], F32)
+        nc.vector.memset(freq[:, 0:1], 1.0)
+        for doubling in range(5):
+            n = 2**doubling
+            nc.vector.tensor_scalar_mul(out=freq[:, n : 2 * n], in0=freq[:, 0:n], scalar1=10000.0 ** (-n / HALF))
+        angle = const.tile([P, 2, HALF], F32)
+        nc.vector.tensor_scalar(out=angle[:, 0, :], in0=freq[:], scalar1=pos[:, 0:1], scalar2=None, op0=ALU.mult)
+        nc.vector.tensor_scalar(
+            out=angle[:, 1, :], in0=freq[:], scalar1=pos[:, 0:1], scalar2=math.pi / 2, op0=ALU.mult, op1=ALU.add
+        )
+        turns_int = const.tile([P, 2, HALF], I32)
+        nc.vector.tensor_scalar(out=turns_int[:], in0=angle[:], scalar1=0.5 / math.pi, scalar2=None, op0=ALU.mult)
+        turns = const.tile([P, 2, HALF], F32)
+        nc.vector.tensor_copy(out=turns[:], in_=turns_int[:])
+        rest = const.tile([P, 2, HALF], F32)
+        nc.vector.scalar_tensor_tensor(
+            out=rest[:], in0=turns[:], scalar=-2.0 * math.pi, in1=angle[:], op0=ALU.mult, op1=ALU.add
+        )
+        one_more = const.tile([P, 2, HALF], F32)
+        nc.vector.tensor_scalar(
+            out=one_more[:], in0=rest[:], scalar1=math.pi, scalar2=-2.0 * math.pi, op0=ALU.is_gt, op1=ALU.mult
+        )
+        nc.vector.tensor_tensor(out=rest[:], in0=rest[:], in1=one_more[:], op=ALU.add)
+        sin_cos = const.tile([P, 2, HALF], F32)
+        nc.scalar.activation(out=sin_cos[:], in_=rest[:], func=ACT.Sin)
+        minus_sin = const.tile([P, HALF], F32)
+        nc.vector.tensor_scalar_mul(out=minus_sin[:], in0=sin_cos[:, 0, :], scalar1=-1.0)
+        sin = sin_cos[:, 0, :]
+        cos = sin_cos[:, 1, :]
+
+        def quantise(grouped, i, c):
+            groups = slice(CHUNK_GROUPS * c, CHUNK_GROUPS * (c + 1))
+            nc.vector.quantize_mx(
+                out=codes[i][:, groups, :].rearrange("p g m -> p (g m)").bitcast(FP8X4),
+                scales=code_planes[i][:, groups, :].rearrange("p g m -> p (g m)"),
+                in_=grouped[:].rearrange("p g m t -> p (g m t)"),
+            )
+
+        def transpose_cached(i, c):
+            words = cached[(i, c)][:].bitcast(F32)
+            grouped = stage.tile([P, CHUNK_GROUPS, P, PACK], BF16, align_bytes=64, tag="grouped", bufs=3)
+            grouped_words = grouped[:].bitcast(F32)
+            for half in range(2):
+                bank = banks.tile([P, 2, 2, P], F32, tag="turned")
+                for g in range(2):
+                    first = (GROUP // 2) * (2 * half + g)
+                    for u in range(2):
+                        nc.tensor.transpose(
+                            bank[:, g, u, :], words[:, first + u : first + GROUP // 2 : 2], identity[:]
+                        )
+                nc.scalar.copy(
+                    out=grouped_words[:, 2 * half : 2 * half + 2, :, :], in_=bank[:].rearrange("p g u m -> p g m u")
+                )
+            quantise(grouped, i, c)
+
+        def mx_pass(acc, i, w, g):
+            nc.tensor.matmul_mx(
+                out=acc[:],
+                lhsT=codes[i][:, g, :].bitcast(FP8X4),
+                lhsT_scale=code_planes[i][:, g, :],
+                rhs=weight_words[w][g].bitcast(FP8X4),
+                rhs_scale=weight_planes[w][g],
+                start=(g == 0),
+                stop=(g == GROUPS - 1),
+            )
+
+        def chunk_passes(acc, i, w, c):
+            for g in range(CHUNK_GROUPS * c, CHUNK_GROUPS * (c + 1)):
+                mx_pass(acc, i, w, g)
+
+        def store_tile(rows, i, result):
+            for b in range(BATCH):
+                nc.sync.dma_start(out=rows[b, SEQ * i : SEQ * (i + 1), :], in_=result[SEQ * b : SEQ * (b + 1), :])
+
+        def rotary(source):
+            x = source.rearrange("p (h two i) -> p h two i", two=2, i=HALF)
+            direct = stage.tile([P, HEADS, 2, HALF], F32, tag="direct", bufs=3)
+            crossed = stage.tile([P, HEADS, 2, HALF], F32, tag="crossed")
+            nc.vector.tensor_tensor(
+                out=direct[:].rearrange("p h two i -> p (h two) i"),
+                in0=source.rearrange("p (j i) -> p j i", i=HALF),
+                in1=cos.unsqueeze(1).to_broadcast([P, 2 * HEADS, HALF]),
+                op=ALU.mult,
+            )
+            nc.vector.tensor_tensor(
+                out=crossed[:, :, 0, :],
+                in0=x[:, :, 1, :],
+                in1=minus_sin[:].unsqueeze(1).to_broadcast([P, HEADS, HALF]),
+                op=ALU.mult,
+            )
+            nc.vector.tensor_tensor(
+                out=crossed[:, :, 1, :],
+                in0=x[:, :, 0, :],
+                in1=sin.unsqueeze(1).to_broadcast([P, HEADS, HALF]),
+                op=ALU.mult,
+            )
+            nc.vector.tensor_tensor(out=direct[:], in0=direct[:], in1=crossed[:], op=ALU.add)
+            return direct[:].rearrange("p h two i -> p (h two i)")
+
+        stats = const.tile([P, GROUPS, 6], F32)
+        key_acc = [banks.tile([P, COLS], F32, tag="acc", name="key_acc") for i in range(LAYERS)]
+        key_raw = {}
+
+        def key_passes(step):
+            c, pair = divmod(step, LAYERS // PAIR)
+            for i in range(PAIR * pair, PAIR * (pair + 1)):
+                chunk_passes(key_acc[i], i, "k", c)
+                if c == CHUNKS - 1:
+                    key_raw[i] = stage.tile([P, COLS], F32, tag="key_raw", bufs=LAYERS, name="key_raw")
+                    nc.scalar.copy(out=key_raw[i][:], in_=key_acc[i][:])
+
+        for step in range(STEPS):
+            c, pair = divmod(step, LAYERS // PAIR)
+            for i in range(PAIR * pair, PAIR * (pair + 1)):
+                transpose_cached(i, c)
+            if step >= 1:
+                key_passes(step - 1)
+            if step + AHEAD < STEPS:
+                load_step(step + AHEAD)
+            else:
+                if step + AHEAD == STEPS:
+                    for c_v in range(CHUNKS):
+                        load_resident_chunk("v", c_v)
+                    for c_q in range(CHUNKS):
+                        load_scales("q", c_q)
+                for j in range(PAIR):
+                    q_words = ring.tile([P, 2, COLS], U32, align_bytes=64, tag="ring", name="q_words")
+                    load_words("q", q_words, len(weight_words["q"]), 2)
+            if STATS_STEP <= step < STATS_STEP + CHUNKS:
+                for g in range(CHUNK_GROUPS * (step - STATS_STEP), CHUNK_GROUPS * (step - STATS_STEP + 1)):
+                    nc.vector.bn_stats(out=stats[:, g, :], in_=hidden_raw[:, GROUP * g : GROUP * (g + 1)])
+
+        mean_var = const.tile([P, 2], F32)
+        nc.vector.bn_aggr(out=mean_var[:], in_=stats[:].rearrange("p g s -> p (g s)"))
+        var_eps = const.tile([P, 1], F32)
+        nc.vector.tensor_scalar_add(out=var_eps[:], in0=mean_var[:, 1:2], scalar1=EPS)
+        std = const.tile([P, 1], F32)
+        nc.scalar.sqrt(out=std[:], in_=var_eps[:])
+        rstd = const.tile([P, 1], F32)
+        nc.vector.reciprocal(out=rstd[:], in_=std[:])
+        minus_mean_rstd = const.tile([P, 1], F32)
+        nc.vector.scalar_tensor_tensor(
+            out=minus_mean_rstd[:], in0=mean_var[:, 0:1], scalar=-1.0, in1=rstd[:], op0=ALU.mult, op1=ALU.mult
+        )
+
+        key_passes(STEPS - 1)
+
+        centred = {}
+
+        def centre(c):
+            centred[c] = stage.tile([P, CHUNK_GROUPS, PACK, P], F32, tag="centred", name="centred")
+            nc.scalar.activation(
+                out=centred[c][:],
+                in_=hidden_raw[:, CHUNK * c : CHUNK * (c + 1)].rearrange("m (g p t) -> m g t p", g=CHUNK_GROUPS, t=PACK),
+                func=ACT.Identity,
+                scale=rstd[:, 0:1],
+                bias=minus_mean_rstd[:, 0:1],
+            )
+
+        centre(0)
+        centre(1)
+
+        for i in range(PAIR):
+            store_tile(k_rows, i, rotary(key_raw[i][:]))
+
+        gain_bias = const.tile([P, 2 * GROUPS, PACK], F32)
+
+        def spread_gain_bias():
+            row_words = gain_bias_rows[:].bitcast(F32)
+            bank = banks.tile([P, 2, P], F32, tag="turned")
+            for u in range(2):
+                nc.tensor.transpose(bank[:, u, :], row_words[:, u : GROUP // 2 : 2], identity[:])
+            nc.vector.tensor_copy(
+                out=gain_bias[:].rearrange("p r (u e) -> p r u e", u=2),
+                in_=bank[:].bitcast(BF16).rearrange("p u (r e) -> p r u e", e=2)[:, 0 : 2 * GROUPS, :, :],
+            )
+
+        def finish_normed(c):
+            scaled = stage.tile([P, CHUNK_GROUPS, P, PACK], F32, tag="scaled", bufs=1)
+            for g in range(CHUNK_GROUPS):
+                bank = banks.tile([P, PACK, P], F32, tag="turned")
+                for t in range(PACK):
+                    nc.tensor.transpose(bank[:, t, :], centred[c][:, g, t, :], identity[:])
+                nc.vector.tensor_tensor(
+                    out=scaled[:, g, :, :],
+                    in0=bank[:].rearrange("p t m -> p m t"),
+                    in1=gain_bias[:, CHUNK_GROUPS * c + g, :].unsqueeze(1).to_broadcast([P, P, PACK]),
+                    op=ALU.mult,
+                )
+            grouped = stage.tile([P, CHUNK_GROUPS, P, PACK], BF16, align_bytes=64, tag="grouped", bufs=3)
+            first = GROUPS + CHUNK_GROUPS * c
+            nc.vector.tensor_tensor(
+                out=grouped[:],
+                in0=scaled[:],
+                in1=gain_bias[:, first : first + CHUNK_GROUPS, :].unsqueeze(2).to_broadcast([P, CHUNK_GROUPS, P, PACK]),
+                op=ALU.add,
+            )
+            quantise(grouped, HIDDEN, c)
+
+        value_acc = [banks.tile([P, COLS], F32, tag="acc", name="value_acc") for i in range(LAYERS)]
+        for c in range(CHUNKS):
+            for i in range(LAYERS):
+                chunk_passes(value_acc[i], i, "v", c)
+                if c == CHUNKS - 1:
+                    value = stage.tile([P, COLS], F32, tag="value", bufs=3)
+                    nc.scalar.copy(out=value[:], in_=value_acc[i][:])
+                    store_tile(v_rows, i, value[:])
+            if c == 0:
+                spread_gain_bias()
+            finish_normed(c)
+            if c + 2 < CHUNKS:
+                centre(c + 2)
+
+        for i in range(PAIR, LAYERS):
+            store_tile(k_rows, i, rotary(key_raw[i][:]))
+
+        hidden_acc = {}
+        for w in ("q", "k", "v"):
+            hidden_acc[w] = banks.tile([P, COLS], F32, tag="acc", name="hidden_acc")
+        for c in range(CHUNKS):
+            for w in ("q", "k", "v"):
+                chunk_passes(hidden_acc[w], HIDDEN, w, c)
+        nc.sync.dma_start(out=q_rows, in_=rotary(hidden_acc["q"][:]))
+        store_tile(k_rows, HIDDEN, rotary(hidden_acc["k"][:]))
+        value = stage.tile([P, COLS], F32, tag="value", bufs=3)
+        nc.scalar.copy(out=value[:], in_=hidden_acc["v"][:])
+        store_tile(v_rows, HIDDEN, value[:])

@@ -32,9 +32,10 @@ EPS = 1e-5
 QUADRANTS = 4
 PAIR = 2
 STEPS = CHUNKS * LAYERS // PAIR
-RING = 8
+RING = 4
 AHEAD = RING // PAIR
-STATS_STEP = 3
+STATS_STEP = 2
+STATS_GROUPS = 2
 
 FLOPS = 2 * FEATURES * COLS * (P + 2 * (LAYERS + 1) * P)
 
@@ -118,11 +119,16 @@ def tile_mlablock_pa_k_kernel(
             if pair == 0:
                 load_scales("k", c)
             for i in range(PAIR * pair, PAIR * (pair + 1)):
-                cached[(i, c)] = ring.tile([P, CHUNK], BF16, align_bytes=64, tag="ring", name="cached")
+                cached[(i, c)] = ring.tile([P, CHUNK], BF16, align_bytes=64, tag="raw", name="cached")
                 nc.sync.dma_start(out=cached[(i, c)][:], in_=cache_rows[i, :, CHUNK * c : CHUNK * (c + 1)])
             if pair == 0:
                 chunk_words = keep.tile([P, CHUNK_GROUPS, COLS], U32, align_bytes=64, name="words_k%d" % c)
                 load_words("k", chunk_words, CHUNK_GROUPS * c, CHUNK_GROUPS)
+
+        def load_query_words(tag):
+            for j in range(PAIR):
+                q_words = ring.tile([P, 2, COLS], U32, align_bytes=64, tag=tag, name="q_words")
+                load_words("q", q_words, len(weight_words["q"]), 2)
 
         for step in range(AHEAD):
             load_step(step)
@@ -175,18 +181,27 @@ def tile_mlablock_pa_k_kernel(
                 in_=grouped[:].rearrange("p g m t -> p (g m t)"),
             )
 
+        sorted_words = {}
+
+        def sort_step(step):
+            c, pair = divmod(step, LAYERS // PAIR)
+            for i in range(PAIR * pair, PAIR * (pair + 1)):
+                sorted_words[(i, c)] = ring.tile(
+                    [P, CHUNK_GROUPS, 2, P], F32, align_bytes=64, tag="sorted", name="sorted_words"
+                )
+                nc.vector.tensor_copy(
+                    out=sorted_words[(i, c)][:],
+                    in_=cached[(i, c)][:].bitcast(F32).rearrange("m (g p u) -> m g u p", g=CHUNK_GROUPS, u=2),
+                )
+
         def transpose_cached(i, c):
-            words = cached[(i, c)][:].bitcast(F32)
             grouped = stage.tile([P, CHUNK_GROUPS, P, PACK], BF16, align_bytes=64, tag="grouped", bufs=3)
             grouped_words = grouped[:].bitcast(F32)
             for half in range(2):
                 bank = banks.tile([P, 2, 2, P], F32, tag="turned")
                 for g in range(2):
-                    first = (GROUP // 2) * (2 * half + g)
                     for u in range(2):
-                        nc.tensor.transpose(
-                            bank[:, g, u, :], words[:, first + u : first + GROUP // 2 : 2], identity[:]
-                        )
+                        nc.tensor.transpose(bank[:, g, u, :], sorted_words[(i, c)][:, 2 * half + g, u, :], identity[:])
                 nc.scalar.copy(
                     out=grouped_words[:, 2 * half : 2 * half + 2, :, :], in_=bank[:].rearrange("p g u m -> p g m u")
                 )
@@ -248,12 +263,8 @@ def tile_mlablock_pa_k_kernel(
                     key_raw[i] = stage.tile([P, COLS], F32, tag="key_raw", bufs=LAYERS, name="key_raw")
                     nc.scalar.copy(out=key_raw[i][:], in_=key_acc[i][:])
 
-        for step in range(STEPS):
-            c, pair = divmod(step, LAYERS // PAIR)
-            for i in range(PAIR * pair, PAIR * (pair + 1)):
-                transpose_cached(i, c)
-            if step >= 1:
-                key_passes(step - 1)
+        def sort_and_refill(step):
+            sort_step(step)
             if step + AHEAD < STEPS:
                 load_step(step + AHEAD)
             else:
@@ -262,12 +273,26 @@ def tile_mlablock_pa_k_kernel(
                         load_resident_chunk("v", c_v)
                     for c_q in range(CHUNKS):
                         load_scales("q", c_q)
-                for j in range(PAIR):
-                    q_words = ring.tile([P, 2, COLS], U32, align_bytes=64, tag="ring", name="q_words")
-                    load_words("q", q_words, len(weight_words["q"]), 2)
-            if STATS_STEP <= step < STATS_STEP + CHUNKS:
-                for g in range(CHUNK_GROUPS * (step - STATS_STEP), CHUNK_GROUPS * (step - STATS_STEP + 1)):
-                    nc.vector.bn_stats(out=stats[:, g, :], in_=hidden_raw[:, GROUP * g : GROUP * (g + 1)])
+                load_query_words("raw")
+
+        def take_stats(first, last):
+            for g in range(first, last):
+                nc.vector.bn_stats(out=stats[:, g, :], in_=hidden_raw[:, GROUP * g : GROUP * (g + 1)])
+
+        sort_and_refill(0)
+        for step in range(STEPS):
+            if step + 1 < STEPS:
+                sort_and_refill(step + 1)
+            c, pair = divmod(step, LAYERS // PAIR)
+            for i in range(PAIR * pair, PAIR * (pair + 1)):
+                transpose_cached(i, c)
+            if step + AHEAD >= STEPS:
+                load_query_words("sorted")
+            if step >= 1:
+                key_passes(step - 1)
+            if step >= STATS_STEP:
+                take_stats(STATS_GROUPS * (step - STATS_STEP), STATS_GROUPS * (step - STATS_STEP + 1))
+        take_stats(STATS_GROUPS * (STEPS - STATS_STEP), GROUPS)
 
         mean_var = const.tile([P, 2], F32)
         nc.vector.bn_aggr(out=mean_var[:], in_=stats[:].rearrange("p g s -> p (g s)"))

@@ -35,7 +35,7 @@ STEPS = CHUNKS * LAYERS // PAIR
 RING = 4
 AHEAD = RING // PAIR
 STATS_STEP = 2
-STATS_GROUPS = 2
+STATS_GROUPS = 3
 
 FLOPS = 2 * FEATURES * COLS * (P + 2 * (LAYERS + 1) * P)
 
@@ -157,21 +157,23 @@ def tile_mlablock_pa_k_kernel(
         nc.vector.tensor_scalar(out=turns_int[:], in0=angle[:], scalar1=0.5 / math.pi, scalar2=None, op0=ALU.mult)
         turns = const.tile([P, 2, HALF], F32)
         nc.vector.tensor_copy(out=turns[:], in_=turns_int[:])
-        rest = const.tile([P, 2, HALF], F32)
+        rest = const.tile([P, 3, HALF], F32)
         nc.vector.scalar_tensor_tensor(
-            out=rest[:], in0=turns[:], scalar=-2.0 * math.pi, in1=angle[:], op0=ALU.mult, op1=ALU.add
+            out=rest[:, 0:2, :], in0=turns[:], scalar=-2.0 * math.pi, in1=angle[:], op0=ALU.mult, op1=ALU.add
         )
         one_more = const.tile([P, 2, HALF], F32)
         nc.vector.tensor_scalar(
-            out=one_more[:], in0=rest[:], scalar1=math.pi, scalar2=-2.0 * math.pi, op0=ALU.is_gt, op1=ALU.mult
+            out=one_more[:], in0=rest[:, 0:2, :], scalar1=math.pi, scalar2=-2.0 * math.pi, op0=ALU.is_gt, op1=ALU.mult
         )
-        nc.vector.tensor_tensor(out=rest[:], in0=rest[:], in1=one_more[:], op=ALU.add)
-        sin_cos = const.tile([P, 2, HALF], F32)
-        nc.scalar.activation(out=sin_cos[:], in_=rest[:], func=ACT.Sin)
-        minus_sin = const.tile([P, HALF], F32)
-        nc.vector.tensor_scalar_mul(out=minus_sin[:], in0=sin_cos[:, 0, :], scalar1=-1.0)
-        sin = sin_cos[:, 0, :]
-        cos = sin_cos[:, 1, :]
+        nc.vector.tensor_tensor(out=rest[:, 0:2, :], in0=rest[:, 0:2, :], in1=one_more[:], op=ALU.add)
+        nc.vector.tensor_scalar_mul(out=rest[:, 2, :], in0=rest[:, 0, :], scalar1=-1.0)
+        trig = const.tile([P, 3, HALF], F32)
+        nc.scalar.activation(out=trig[:], in_=rest[:], func=ACT.Sin)
+        sin = trig[:, 0, :]
+        cos = trig[:, 1, :]
+        minus_sin = trig[:, 2, :]
+        table_warmer = const.tile([P, 1], F32)
+        nc.scalar.sqrt(out=table_warmer[:], in_=freq[:, 0:1])
 
         def quantise(grouped, i, c):
             groups = slice(CHUNK_GROUPS * c, CHUNK_GROUPS * (c + 1))
@@ -183,16 +185,14 @@ def tile_mlablock_pa_k_kernel(
 
         sorted_words = {}
 
-        def sort_step(step):
-            c, pair = divmod(step, LAYERS // PAIR)
-            for i in range(PAIR * pair, PAIR * (pair + 1)):
-                sorted_words[(i, c)] = ring.tile(
-                    [P, CHUNK_GROUPS, 2, P], F32, align_bytes=64, tag="sorted", name="sorted_words"
-                )
-                nc.vector.tensor_copy(
-                    out=sorted_words[(i, c)][:],
-                    in_=cached[(i, c)][:].bitcast(F32).rearrange("m (g p u) -> m g u p", g=CHUNK_GROUPS, u=2),
-                )
+        def sort_chunk(copy, i, c):
+            sorted_words[(i, c)] = ring.tile(
+                [P, CHUNK_GROUPS, 2, P], F32, align_bytes=64, tag="sorted", name="sorted_words"
+            )
+            copy(
+                out=sorted_words[(i, c)][:],
+                in_=cached[(i, c)][:].bitcast(F32).rearrange("m (g p u) -> m g u p", g=CHUNK_GROUPS, u=2),
+            )
 
         def transpose_cached(i, c):
             grouped = stage.tile([P, CHUNK_GROUPS, P, PACK], BF16, align_bytes=64, tag="grouped", bufs=3)
@@ -239,7 +239,7 @@ def tile_mlablock_pa_k_kernel(
             nc.vector.tensor_tensor(
                 out=crossed[:, :, 0, :],
                 in0=x[:, :, 1, :],
-                in1=minus_sin[:].unsqueeze(1).to_broadcast([P, HEADS, HALF]),
+                in1=minus_sin.unsqueeze(1).to_broadcast([P, HEADS, HALF]),
                 op=ALU.mult,
             )
             nc.vector.tensor_tensor(
@@ -263,8 +263,7 @@ def tile_mlablock_pa_k_kernel(
                     key_raw[i] = stage.tile([P, COLS], F32, tag="key_raw", bufs=LAYERS, name="key_raw")
                     nc.scalar.copy(out=key_raw[i][:], in_=key_acc[i][:])
 
-        def sort_and_refill(step):
-            sort_step(step)
+        def refill(step):
             if step + AHEAD < STEPS:
                 load_step(step + AHEAD)
             else:
@@ -279,20 +278,27 @@ def tile_mlablock_pa_k_kernel(
             for g in range(first, last):
                 nc.vector.bn_stats(out=stats[:, g, :], in_=hidden_raw[:, GROUP * g : GROUP * (g + 1)])
 
-        sort_and_refill(0)
+        def first_and_second(step):
+            c, pair = divmod(step, LAYERS // PAIR)
+            return (PAIR * pair, c), (PAIR * pair + 1, c)
+
+        sort_chunk(nc.vector.tensor_copy, *first_and_second(0)[0])
+        sort_chunk(nc.scalar.copy, *first_and_second(0)[1])
+        refill(0)
         for step in range(STEPS):
             if step + 1 < STEPS:
-                sort_and_refill(step + 1)
-            c, pair = divmod(step, LAYERS // PAIR)
-            for i in range(PAIR * pair, PAIR * (pair + 1)):
+                sort_chunk(nc.vector.tensor_copy, *first_and_second(step + 1)[0])
+            for i, c in first_and_second(step):
                 transpose_cached(i, c)
+            if step + 1 < STEPS:
+                sort_chunk(nc.scalar.copy, *first_and_second(step + 1)[1])
+                refill(step + 1)
             if step + AHEAD >= STEPS:
                 load_query_words("sorted")
             if step >= 1:
                 key_passes(step - 1)
             if step >= STATS_STEP:
-                take_stats(STATS_GROUPS * (step - STATS_STEP), STATS_GROUPS * (step - STATS_STEP + 1))
-        take_stats(STATS_GROUPS * (STEPS - STATS_STEP), GROUPS)
+                take_stats(STATS_GROUPS * (step - STATS_STEP), min(STATS_GROUPS * (step - STATS_STEP + 1), GROUPS))
 
         mean_var = const.tile([P, 2], F32)
         nc.vector.bn_aggr(out=mean_var[:], in_=stats[:].rearrange("p g s -> p (g s)"))
@@ -340,25 +346,23 @@ def tile_mlablock_pa_k_kernel(
             )
 
         def finish_normed(c):
-            scaled = stage.tile([P, CHUNK_GROUPS, P, PACK], F32, tag="scaled", bufs=1)
+            grouped = stage.tile([P, CHUNK_GROUPS, P, PACK], BF16, align_bytes=64, tag="grouped", bufs=3)
             for g in range(CHUNK_GROUPS):
                 bank = banks.tile([P, PACK, P], F32, tag="turned")
                 for t in range(PACK):
                     nc.tensor.transpose(bank[:, t, :], centred[c][:, g, t, :], identity[:])
-                nc.vector.tensor_tensor(
-                    out=scaled[:, g, :, :],
-                    in0=bank[:].rearrange("p t m -> p m t"),
-                    in1=gain_bias[:, CHUNK_GROUPS * c + g, :].unsqueeze(1).to_broadcast([P, P, PACK]),
-                    op=ALU.mult,
-                )
-            grouped = stage.tile([P, CHUNK_GROUPS, P, PACK], BF16, align_bytes=64, tag="grouped", bufs=3)
-            first = GROUPS + CHUNK_GROUPS * c
-            nc.vector.tensor_tensor(
-                out=grouped[:],
-                in0=scaled[:],
-                in1=gain_bias[:, first : first + CHUNK_GROUPS, :].unsqueeze(2).to_broadcast([P, CHUNK_GROUPS, P, PACK]),
-                op=ALU.add,
-            )
+                turned = stage.tile([P, PACK, P], F32, tag="turned_copy", bufs=CHUNK_GROUPS)
+                nc.scalar.copy(out=turned[:], in_=bank[:])
+                row = CHUNK_GROUPS * c + g
+                for t in range(PACK):
+                    nc.vector.tensor_scalar(
+                        out=grouped[:, g, :, t],
+                        in0=turned[:, t, :],
+                        scalar1=gain_bias[:, row, t : t + 1],
+                        scalar2=gain_bias[:, GROUPS + row, t : t + 1],
+                        op0=ALU.mult,
+                        op1=ALU.add,
+                    )
             quantise(grouped, HIDDEN, c)
 
         value_acc = [banks.tile([P, COLS], F32, tag="acc", name="value_acc") for i in range(LAYERS)]
@@ -382,8 +386,10 @@ def tile_mlablock_pa_k_kernel(
         for w in ("q", "k", "v"):
             hidden_acc[w] = banks.tile([P, COLS], F32, tag="acc", name="hidden_acc")
         for c in range(CHUNKS):
-            for w in ("q", "k", "v"):
+            for w in ("q", "k"):
                 chunk_passes(hidden_acc[w], HIDDEN, w, c)
+        for c in range(CHUNKS):
+            chunk_passes(hidden_acc["v"], HIDDEN, "v", c)
         nc.sync.dma_start(out=q_rows, in_=rotary(hidden_acc["q"][:]))
         store_tile(k_rows, HIDDEN, rotary(hidden_acc["k"][:]))
         value = stage.tile([P, COLS], F32, tag="value", bufs=3)

@@ -34,8 +34,11 @@ PAIR = 2
 STEPS = CHUNKS * LAYERS // PAIR
 RING = 4
 AHEAD = RING // PAIR
-STATS_STEP = 2
-STATS_GROUPS = 3
+HIDDEN_STEP = STEPS - CHUNKS
+STATS_STEP = HIDDEN_STEP + 1
+STATS_GROUPS = 4
+
+SCALAR_GROUPS = 3
 
 FLOPS = 2 * FEATURES * COLS * (P + 2 * (LAYERS + 1) * P)
 
@@ -76,9 +79,12 @@ def tile_mlablock_pa_k_kernel(
         plane_tiles = {}
         for w in ("k", "v", "q"):
             plane_tiles[w] = keep.tile([P, CHUNKS, COLS], U8, align_bytes=64, name="planes_" + w)
-            nc.vector.memset(plane_tiles[w][:].bitcast(I32), 0)
+        identity = const.tile([P, P], F32)
+        make_identity(nc, identity[:])
+        for w in ("k", "v", "q"):
+            nc.gpsimd.memset(plane_tiles[w][:].bitcast(I32), 0)
         gain_bias_rows = const.tile([P, GROUP], BF16)
-        nc.vector.memset(gain_bias_rows[:], 0.0)
+        nc.gpsimd.memset(gain_bias_rows[:], 0.0)
 
         codes = [keep.tile([P, GROUPS, P], U32, align_bytes=64, name="codes%d" % i) for i in range(LAYERS + 1)]
         code_planes = [keep.tile([P, GROUPS, P], U8, align_bytes=64, name="cplanes%d" % i) for i in range(LAYERS + 1)]
@@ -86,8 +92,10 @@ def tile_mlablock_pa_k_kernel(
         weight_words = {"q": [], "k": [], "v": []}
         weight_planes = {"q": [], "k": [], "v": []}
 
-        identity = const.tile([P, P], F32)
-        make_identity(nc, identity[:])
+        one = const.tile([P, 1], F32)
+        nc.vector.memset(one[:], 1.0)
+        table_warmer = const.tile([P, 1], F32)
+        nc.scalar.activation(out=table_warmer[:], in_=one[:], func=ACT.Sin)
 
         def load_scales(w, c):
             for quadrant in range(QUADRANTS):
@@ -116,64 +124,32 @@ def tile_mlablock_pa_k_kernel(
 
         def load_step(step):
             c, pair = divmod(step, LAYERS // PAIR)
-            if pair == 0:
-                load_scales("k", c)
             for i in range(PAIR * pair, PAIR * (pair + 1)):
                 cached[(i, c)] = ring.tile([P, CHUNK], BF16, align_bytes=64, tag="raw", name="cached")
-                nc.sync.dma_start(out=cached[(i, c)][:], in_=cache_rows[i, :, CHUNK * c : CHUNK * (c + 1)])
+                pieces = 2 if step == 0 else 1
+                width = CHUNK // pieces
+                for piece in range(pieces):
+                    nc.sync.dma_start(
+                        out=cached[(i, c)][:, width * piece : width * (piece + 1)],
+                        in_=cache_rows[i, :, CHUNK * c + width * piece : CHUNK * c + width * (piece + 1)],
+                    )
             if pair == 0:
+                load_scales("k", c)
                 chunk_words = keep.tile([P, CHUNK_GROUPS, COLS], U32, align_bytes=64, name="words_k%d" % c)
                 load_words("k", chunk_words, CHUNK_GROUPS * c, CHUNK_GROUPS)
+
+            if step >= HIDDEN_STEP:
+                part = slice(CHUNK * (step - HIDDEN_STEP), CHUNK * (step - HIDDEN_STEP + 1))
+                nc.sync.dma_start(out=hidden_raw[:, part], in_=hidden_rows[:, part])
 
         def load_query_words(tag):
             for j in range(PAIR):
                 q_words = ring.tile([P, 2, COLS], U32, align_bytes=64, tag=tag, name="q_words")
                 load_words("q", q_words, len(weight_words["q"]), 2)
 
+        hidden_raw = keep.tile([P, FEATURES], BF16)
         for step in range(AHEAD):
             load_step(step)
-        hidden_raw = keep.tile([P, FEATURES], BF16)
-        nc.sync.dma_start(out=hidden_raw[:], in_=hidden_rows)
-        nc.sync.dma_start(out=gain_bias_rows[0:GROUPS, :], in_=ln_scale.rearrange("(g k) -> g k", k=GROUP))
-        nc.sync.dma_start(out=gain_bias_rows[GROUPS : 2 * GROUPS, :], in_=ln_bias.rearrange("(g k) -> g k", k=GROUP))
-
-        partition_index = const.tile([P, 1], I32)
-        nc.gpsimd.iota(partition_index[:], pattern=[[0, 1]], base=0, channel_multiplier=1)
-        pos_int = const.tile([P, 1], I32)
-        nc.vector.tensor_single_scalar(out=pos_int[:], in_=partition_index[:], scalar=SEQ - 1, op=ALU.bitwise_and)
-        pos = const.tile([P, 1], F32)
-        nc.vector.tensor_copy(out=pos[:], in_=pos_int[:])
-        freq = const.tile([P, HALF], F32)
-        nc.vector.memset(freq[:, 0:1], 1.0)
-        for doubling in range(5):
-            n = 2**doubling
-            nc.vector.tensor_scalar_mul(out=freq[:, n : 2 * n], in0=freq[:, 0:n], scalar1=10000.0 ** (-n / HALF))
-        angle = const.tile([P, 2, HALF], F32)
-        nc.vector.tensor_scalar(out=angle[:, 0, :], in0=freq[:], scalar1=pos[:, 0:1], scalar2=None, op0=ALU.mult)
-        nc.vector.tensor_scalar(
-            out=angle[:, 1, :], in0=freq[:], scalar1=pos[:, 0:1], scalar2=math.pi / 2, op0=ALU.mult, op1=ALU.add
-        )
-        turns_int = const.tile([P, 2, HALF], I32)
-        nc.vector.tensor_scalar(out=turns_int[:], in0=angle[:], scalar1=0.5 / math.pi, scalar2=None, op0=ALU.mult)
-        turns = const.tile([P, 2, HALF], F32)
-        nc.vector.tensor_copy(out=turns[:], in_=turns_int[:])
-        rest = const.tile([P, 3, HALF], F32)
-        nc.vector.scalar_tensor_tensor(
-            out=rest[:, 0:2, :], in0=turns[:], scalar=-2.0 * math.pi, in1=angle[:], op0=ALU.mult, op1=ALU.add
-        )
-        one_more = const.tile([P, 2, HALF], F32)
-        nc.vector.tensor_scalar(
-            out=one_more[:], in0=rest[:, 0:2, :], scalar1=math.pi, scalar2=-2.0 * math.pi, op0=ALU.is_gt, op1=ALU.mult
-        )
-        nc.vector.tensor_tensor(out=rest[:, 0:2, :], in0=rest[:, 0:2, :], in1=one_more[:], op=ALU.add)
-        nc.vector.tensor_scalar_mul(out=rest[:, 2, :], in0=rest[:, 0, :], scalar1=-1.0)
-        trig = const.tile([P, 3, HALF], F32)
-        nc.scalar.activation(out=trig[:], in_=rest[:], func=ACT.Sin)
-        sin = trig[:, 0, :]
-        cos = trig[:, 1, :]
-        minus_sin = trig[:, 2, :]
-        table_warmer = const.tile([P, 1], F32)
-        nc.scalar.sqrt(out=table_warmer[:], in_=freq[:, 0:1])
 
         def quantise(grouped, i, c):
             groups = slice(CHUNK_GROUPS * c, CHUNK_GROUPS * (c + 1))
@@ -185,14 +161,15 @@ def tile_mlablock_pa_k_kernel(
 
         sorted_words = {}
 
-        def sort_chunk(copy, i, c):
+        def sort_chunk(copy, i, c, pieces=1):
             sorted_words[(i, c)] = ring.tile(
                 [P, CHUNK_GROUPS, 2, P], F32, align_bytes=64, tag="sorted", name="sorted_words"
             )
-            copy(
-                out=sorted_words[(i, c)][:],
-                in_=cached[(i, c)][:].bitcast(F32).rearrange("m (g p u) -> m g u p", g=CHUNK_GROUPS, u=2),
-            )
+            source = cached[(i, c)][:].bitcast(F32).rearrange("m (g p u) -> m g u p", g=CHUNK_GROUPS, u=2)
+            groups = CHUNK_GROUPS // pieces
+            for piece in range(pieces):
+                part = slice(groups * piece, groups * (piece + 1))
+                copy(out=sorted_words[(i, c)][:, part], in_=source[:, part])
 
         def transpose_cached(i, c):
             grouped = stage.tile([P, CHUNK_GROUPS, P, PACK], BF16, align_bytes=64, tag="grouped", bufs=3)
@@ -268,11 +245,52 @@ def tile_mlablock_pa_k_kernel(
                 load_step(step + AHEAD)
             else:
                 if step + AHEAD == STEPS:
+                    nc.sync.dma_start(out=gain_bias_rows[0:GROUPS, :], in_=ln_scale.rearrange("(g k) -> g k", k=GROUP))
+                    nc.sync.dma_start(
+                        out=gain_bias_rows[GROUPS : 2 * GROUPS, :], in_=ln_bias.rearrange("(g k) -> g k", k=GROUP)
+                    )
                     for c_v in range(CHUNKS):
                         load_resident_chunk("v", c_v)
                     for c_q in range(CHUNKS):
                         load_scales("q", c_q)
                 load_query_words("raw")
+
+        partition_index = const.tile([P, 1], I32)
+        pos_int = const.tile([P, 1], I32)
+        pos = const.tile([P, 1], F32)
+        freq = const.tile([P, HALF], F32)
+        angle = const.tile([P, 2, HALF], F32)
+        turns_int = const.tile([P, 2, HALF], I32)
+        turns = const.tile([P, 2, HALF], F32)
+        rest = const.tile([P, 3, HALF], F32)
+        one_more = const.tile([P, 2, HALF], F32)
+        trig = const.tile([P, 3, HALF], F32)
+        sin = trig[:, 0, :]
+        cos = trig[:, 1, :]
+        minus_sin = trig[:, 2, :]
+
+        def rotary_angles():
+            nc.gpsimd.iota(partition_index[:], pattern=[[0, 1]], base=0, channel_multiplier=1)
+            nc.vector.tensor_single_scalar(out=pos_int[:], in_=partition_index[:], scalar=SEQ - 1, op=ALU.bitwise_and)
+            nc.vector.tensor_copy(out=pos[:], in_=pos_int[:])
+            nc.vector.memset(freq[:, 0:1], 1.0)
+            for doubling in range(5):
+                n = 2**doubling
+                nc.vector.tensor_scalar_mul(out=freq[:, n : 2 * n], in0=freq[:, 0:n], scalar1=10000.0 ** (-n / HALF))
+            nc.vector.tensor_scalar(out=angle[:, 0, :], in0=freq[:], scalar1=pos[:, 0:1], scalar2=None, op0=ALU.mult)
+            nc.vector.tensor_scalar(
+                out=angle[:, 1, :], in0=freq[:], scalar1=pos[:, 0:1], scalar2=math.pi / 2, op0=ALU.mult, op1=ALU.add
+            )
+            nc.vector.tensor_scalar(out=turns_int[:], in0=angle[:], scalar1=0.5 / math.pi, scalar2=None, op0=ALU.mult)
+            nc.vector.tensor_copy(out=turns[:], in_=turns_int[:])
+            nc.vector.scalar_tensor_tensor(
+                out=rest[:, 0:2, :], in0=turns[:], scalar=-2.0 * math.pi, in1=angle[:], op0=ALU.mult, op1=ALU.add
+            )
+            nc.vector.tensor_scalar(
+                out=one_more[:], in0=rest[:, 0:2, :], scalar1=math.pi, scalar2=-2.0 * math.pi, op0=ALU.is_gt, op1=ALU.mult
+            )
+            nc.vector.tensor_tensor(out=rest[:, 0:2, :], in0=rest[:, 0:2, :], in1=one_more[:], op=ALU.add)
+            nc.vector.tensor_scalar_mul(out=rest[:, 2, :], in0=rest[:, 0, :], scalar1=-1.0)
 
         def take_stats(first, last):
             for g in range(first, last):
@@ -282,8 +300,8 @@ def tile_mlablock_pa_k_kernel(
             c, pair = divmod(step, LAYERS // PAIR)
             return (PAIR * pair, c), (PAIR * pair + 1, c)
 
-        sort_chunk(nc.vector.tensor_copy, *first_and_second(0)[0])
-        sort_chunk(nc.scalar.copy, *first_and_second(0)[1])
+        sort_chunk(nc.vector.tensor_copy, *first_and_second(0)[0], pieces=2)
+        sort_chunk(nc.vector.tensor_copy, *first_and_second(0)[1], pieces=2)
         refill(0)
         for step in range(STEPS):
             if step + 1 < STEPS:
@@ -299,6 +317,14 @@ def tile_mlablock_pa_k_kernel(
                 key_passes(step - 1)
             if step >= STATS_STEP:
                 take_stats(STATS_GROUPS * (step - STATS_STEP), min(STATS_GROUPS * (step - STATS_STEP + 1), GROUPS))
+            if step == 1:
+                rotary_angles()
+            if step == 3:
+                nc.scalar.activation(out=trig[:], in_=rest[:], func=ACT.Sin)
+        take_stats(STATS_GROUPS * (STEPS - STATS_STEP), GROUPS)
+
+        key_passes(STEPS - 1)
+        nc.scalar.sqrt(out=table_warmer[:], in_=one[:])
 
         mean_var = const.tile([P, 2], F32)
         nc.vector.bn_aggr(out=mean_var[:], in_=stats[:].rearrange("p g s -> p (g s)"))
@@ -312,8 +338,6 @@ def tile_mlablock_pa_k_kernel(
         nc.vector.scalar_tensor_tensor(
             out=minus_mean_rstd[:], in0=mean_var[:, 0:1], scalar=-1.0, in1=rstd[:], op0=ALU.mult, op1=ALU.mult
         )
-
-        key_passes(STEPS - 1)
 
         centred = {}
 
@@ -346,23 +370,30 @@ def tile_mlablock_pa_k_kernel(
             )
 
         def finish_normed(c):
-            grouped = stage.tile([P, CHUNK_GROUPS, P, PACK], BF16, align_bytes=64, tag="grouped", bufs=3)
+            planar = stage.tile([P, CHUNK_GROUPS, PACK, P], BF16, align_bytes=64, tag="planar")
             for g in range(CHUNK_GROUPS):
                 bank = banks.tile([P, PACK, P], F32, tag="turned")
                 for t in range(PACK):
                     nc.tensor.transpose(bank[:, t, :], centred[c][:, g, t, :], identity[:])
-                turned = stage.tile([P, PACK, P], F32, tag="turned_copy", bufs=CHUNK_GROUPS)
-                nc.scalar.copy(out=turned[:], in_=bank[:])
                 row = CHUNK_GROUPS * c + g
                 for t in range(PACK):
-                    nc.vector.tensor_scalar(
-                        out=grouped[:, g, :, t],
-                        in0=turned[:, t, :],
-                        scalar1=gain_bias[:, row, t : t + 1],
-                        scalar2=gain_bias[:, GROUPS + row, t : t + 1],
-                        op0=ALU.mult,
-                        op1=ALU.add,
-                    )
+                    gain = gain_bias[:, row, t : t + 1]
+                    bias = gain_bias[:, GROUPS + row, t : t + 1]
+                    if g < SCALAR_GROUPS:
+                        nc.scalar.activation(
+                            out=planar[:, g, t, :], in_=bank[:, t, :], func=ACT.Identity, scale=gain, bias=bias
+                        )
+                    else:
+                        nc.vector.tensor_scalar(
+                            out=planar[:, g, t, :],
+                            in0=bank[:, t, :],
+                            scalar1=gain,
+                            scalar2=bias,
+                            op0=ALU.mult,
+                            op1=ALU.add,
+                        )
+            grouped = stage.tile([P, CHUNK_GROUPS, P, PACK], BF16, align_bytes=64, tag="grouped", bufs=3)
+            nc.vector.tensor_copy(out=grouped[:], in_=planar[:].rearrange("p g t m -> p g m t"))
             quantise(grouped, HIDDEN, c)
 
         value_acc = [banks.tile([P, COLS], F32, tag="acc", name="value_acc") for i in range(LAYERS)]
@@ -375,12 +406,10 @@ def tile_mlablock_pa_k_kernel(
                     store_tile(v_rows, i, value[:])
             if c == 0:
                 spread_gain_bias()
-            finish_normed(c)
-            if c + 2 < CHUNKS:
-                centre(c + 2)
-
-        for i in range(PAIR, LAYERS):
-            store_tile(k_rows, i, rotary(key_raw[i][:]))
+            else:
+                finish_normed(c - 1)
+                if c + 1 < CHUNKS:
+                    centre(c + 1)
 
         hidden_acc = {}
         for w in ("q", "k", "v"):
@@ -388,6 +417,10 @@ def tile_mlablock_pa_k_kernel(
         for c in range(CHUNKS):
             for w in ("q", "k"):
                 chunk_passes(hidden_acc[w], HIDDEN, w, c)
+            if c == 0:
+                finish_normed(CHUNKS - 1)
+                for i in range(PAIR, LAYERS):
+                    store_tile(k_rows, i, rotary(key_raw[i][:]))
         for c in range(CHUNKS):
             chunk_passes(hidden_acc["v"], HIDDEN, "v", c)
         nc.sync.dma_start(out=q_rows, in_=rotary(hidden_acc["q"][:]))

@@ -32,12 +32,9 @@ EPS = 1e-5
 QUADRANTS = 4
 PAIR = 2
 STEPS = CHUNKS * LAYERS // PAIR
-RING = 4
-AHEAD = RING // PAIR
-HIDDEN_STEP = STEPS - CHUNKS
-STATS_STEP = HIDDEN_STEP + 1
-STATS_GROUPS = 4
-
+RAW_RING = 12
+SORTED_RING = 4
+AHEAD = RAW_RING // PAIR
 SCALAR_GROUPS = 3
 
 FLOPS = 2 * FEATURES * COLS * (P + 2 * (LAYERS + 1) * P)
@@ -63,7 +60,7 @@ def tile_mlablock_pa_k_kernel(
     with ExitStack() as ctx:
         const = ctx.enter_context(tc.tile_pool(name="const", bufs=1))
         keep = ctx.enter_context(tc.tile_pool(name="keep", bufs=1))
-        ring = ctx.enter_context(tc.tile_pool(name="ring", bufs=RING))
+        ring = ctx.enter_context(tc.tile_pool(name="ring", bufs=RAW_RING))
         stage = ctx.enter_context(tc.tile_pool(name="stage", bufs=2))
         banks = ctx.enter_context(tc.psum_pool(name="banks", bufs=4))
         ctx.enter_context(tc.manual_schedule())
@@ -115,11 +112,6 @@ def tile_mlablock_pa_k_kernel(
             for i in range(groups):
                 weight_words[w].append(tile_[:, i, :])
 
-        def load_resident_chunk(w, c):
-            load_scales(w, c)
-            chunk_words = keep.tile([P, CHUNK_GROUPS, COLS], U32, align_bytes=64, name="words_%s%d" % (w, c))
-            load_words(w, chunk_words, CHUNK_GROUPS * c, CHUNK_GROUPS)
-
         cached = {}
 
         def load_step(step):
@@ -133,19 +125,23 @@ def tile_mlablock_pa_k_kernel(
                         out=cached[(i, c)][:, width * piece : width * (piece + 1)],
                         in_=cache_rows[i, :, CHUNK * c + width * piece : CHUNK * c + width * (piece + 1)],
                     )
-            if pair == 0:
+            if (pair == 0) == (c > 0):
                 load_scales("k", c)
                 chunk_words = keep.tile([P, CHUNK_GROUPS, COLS], U32, align_bytes=64, name="words_k%d" % c)
                 load_words("k", chunk_words, CHUNK_GROUPS * c, CHUNK_GROUPS)
+            if step == STEPS - 1:
+                for quarter in range(CHUNKS):
+                    part = slice(CHUNK * quarter, CHUNK * (quarter + 1))
+                    nc.sync.dma_start(out=hidden_raw[:, part], in_=hidden_rows[:, part])
+                nc.sync.dma_start(out=gain_bias_rows[0:GROUPS, :], in_=ln_scale.rearrange("(g k) -> g k", k=GROUP))
+                nc.sync.dma_start(
+                    out=gain_bias_rows[GROUPS : 2 * GROUPS, :], in_=ln_bias.rearrange("(g k) -> g k", k=GROUP)
+                )
 
-            if step >= HIDDEN_STEP:
-                part = slice(CHUNK * (step - HIDDEN_STEP), CHUNK * (step - HIDDEN_STEP + 1))
-                nc.sync.dma_start(out=hidden_raw[:, part], in_=hidden_rows[:, part])
-
-        def load_query_words(tag):
+        def load_late_words(w, tag, bufs):
             for j in range(PAIR):
-                q_words = ring.tile([P, 2, COLS], U32, align_bytes=64, tag=tag, name="q_words")
-                load_words("q", q_words, len(weight_words["q"]), 2)
+                words = ring.tile([P, 2, COLS], U32, align_bytes=64, tag=tag, bufs=bufs, name="late_words")
+                load_words(w, words, len(weight_words[w]), 2)
 
         hidden_raw = keep.tile([P, FEATURES], BF16)
         for step in range(AHEAD):
@@ -163,7 +159,7 @@ def tile_mlablock_pa_k_kernel(
 
         def sort_chunk(copy, i, c, pieces=1):
             sorted_words[(i, c)] = ring.tile(
-                [P, CHUNK_GROUPS, 2, P], F32, align_bytes=64, tag="sorted", name="sorted_words"
+                [P, CHUNK_GROUPS, 2, P], F32, align_bytes=64, tag="sorted", bufs=SORTED_RING, name="sorted_words"
             )
             source = cached[(i, c)][:].bitcast(F32).rearrange("m (g p u) -> m g u p", g=CHUNK_GROUPS, u=2)
             groups = CHUNK_GROUPS // pieces
@@ -243,17 +239,16 @@ def tile_mlablock_pa_k_kernel(
         def refill(step):
             if step + AHEAD < STEPS:
                 load_step(step + AHEAD)
+                return
+            c = step + AHEAD - STEPS
+            if c < CHUNKS:
+                load_scales("v", c)
+                load_late_words("v", "raw", RAW_RING)
             else:
-                if step + AHEAD == STEPS:
-                    nc.sync.dma_start(out=gain_bias_rows[0:GROUPS, :], in_=ln_scale.rearrange("(g k) -> g k", k=GROUP))
-                    nc.sync.dma_start(
-                        out=gain_bias_rows[GROUPS : 2 * GROUPS, :], in_=ln_bias.rearrange("(g k) -> g k", k=GROUP)
-                    )
-                    for c_v in range(CHUNKS):
-                        load_resident_chunk("v", c_v)
+                if c == CHUNKS:
                     for c_q in range(CHUNKS):
                         load_scales("q", c_q)
-                load_query_words("raw")
+                load_late_words("q", "raw", RAW_RING)
 
         partition_index = const.tile([P, 1], I32)
         pos_int = const.tile([P, 1], I32)
@@ -311,17 +306,17 @@ def tile_mlablock_pa_k_kernel(
             if step + 1 < STEPS:
                 sort_chunk(nc.scalar.copy, *first_and_second(step + 1)[1])
                 refill(step + 1)
-            if step + AHEAD >= STEPS:
-                load_query_words("sorted")
+            if step + PAIR >= STEPS:
+                load_late_words("q", "sorted", SORTED_RING)
             if step >= 1:
                 key_passes(step - 1)
-            if step >= STATS_STEP:
-                take_stats(STATS_GROUPS * (step - STATS_STEP), min(STATS_GROUPS * (step - STATS_STEP + 1), GROUPS))
+            if step == STEPS - 2:
+                take_stats(0, CHUNK_GROUPS)
             if step == 1:
                 rotary_angles()
             if step == 3:
                 nc.scalar.activation(out=trig[:], in_=rest[:], func=ACT.Sin)
-        take_stats(STATS_GROUPS * (STEPS - STATS_STEP), GROUPS)
+        take_stats(CHUNK_GROUPS, GROUPS)
 
         key_passes(STEPS - 1)
         nc.scalar.sqrt(out=table_warmer[:], in_=one[:])

@@ -178,15 +178,15 @@ def tile_mlablock_pa_k_kernel(
                 nc.scalar.copy(
                     out=grouped_words[:, 2 * half : 2 * half + 2, :, :], in_=bank[:].rearrange("p g u m -> p g m u")
                 )
-            quantise(grouped, i, c)
+            return grouped
 
-        def mx_pass(acc, i, w, g):
+        def mx_pass(acc, i, w, g, cols=slice(0, COLS)):
             nc.tensor.matmul_mx(
                 out=acc[:],
                 lhsT=codes[i][:, g, :].bitcast(FP8X4),
                 lhsT_scale=code_planes[i][:, g, :],
-                rhs=weight_words[w][g].bitcast(FP8X4),
-                rhs_scale=weight_planes[w][g],
+                rhs=weight_words[w][g][:, cols].bitcast(FP8X4),
+                rhs_scale=weight_planes[w][g][:, cols],
                 start=(g == 0),
                 stop=(g == GROUPS - 1),
             )
@@ -264,28 +264,47 @@ def tile_mlablock_pa_k_kernel(
         cos = trig[:, 1, :]
         minus_sin = trig[:, 2, :]
 
-        def rotary_angles():
-            nc.gpsimd.iota(partition_index[:], pattern=[[0, 1]], base=0, channel_multiplier=1)
-            nc.vector.tensor_single_scalar(out=pos_int[:], in_=partition_index[:], scalar=SEQ - 1, op=ALU.bitwise_and)
-            nc.vector.tensor_copy(out=pos[:], in_=pos_int[:])
-            nc.vector.memset(freq[:, 0:1], 1.0)
-            for doubling in range(5):
-                n = 2**doubling
-                nc.vector.tensor_scalar_mul(out=freq[:, n : 2 * n], in0=freq[:, 0:n], scalar1=10000.0 ** (-n / HALF))
+        nc.gpsimd.iota(partition_index[:], pattern=[[0, 1]], base=0, channel_multiplier=1)
+        nc.vector.memset(freq[:, 0:1], 1.0)
+
+        def double_freq(n):
+            nc.vector.tensor_scalar_mul(out=freq[:, n : 2 * n], in0=freq[:, 0:n], scalar1=10000.0 ** (-n / HALF))
+
+        def take_angles():
             nc.vector.tensor_scalar(out=angle[:, 0, :], in0=freq[:], scalar1=pos[:, 0:1], scalar2=None, op0=ALU.mult)
             nc.vector.tensor_scalar(
                 out=angle[:, 1, :], in0=freq[:], scalar1=pos[:, 0:1], scalar2=math.pi / 2, op0=ALU.mult, op1=ALU.add
             )
-            nc.vector.tensor_scalar(out=turns_int[:], in0=angle[:], scalar1=0.5 / math.pi, scalar2=None, op0=ALU.mult)
-            nc.vector.tensor_copy(out=turns[:], in_=turns_int[:])
-            nc.vector.scalar_tensor_tensor(
+
+        angle_chain = [
+            lambda: nc.vector.tensor_single_scalar(
+                out=pos_int[:], in_=partition_index[:], scalar=SEQ - 1, op=ALU.bitwise_and
+            ),
+            lambda: nc.vector.tensor_copy(out=pos[:], in_=pos_int[:]),
+            lambda: double_freq(1),
+            lambda: double_freq(2),
+            lambda: double_freq(4),
+            lambda: double_freq(8),
+            lambda: double_freq(16),
+            take_angles,
+            lambda: nc.vector.tensor_scalar(
+                out=turns_int[:], in0=angle[:], scalar1=0.5 / math.pi, scalar2=None, op0=ALU.mult
+            ),
+            lambda: nc.vector.tensor_copy(out=turns[:], in_=turns_int[:]),
+            lambda: nc.vector.scalar_tensor_tensor(
                 out=rest[:, 0:2, :], in0=turns[:], scalar=-2.0 * math.pi, in1=angle[:], op0=ALU.mult, op1=ALU.add
-            )
-            nc.vector.tensor_scalar(
-                out=one_more[:], in0=rest[:, 0:2, :], scalar1=math.pi, scalar2=-2.0 * math.pi, op0=ALU.is_gt, op1=ALU.mult
-            )
-            nc.vector.tensor_tensor(out=rest[:, 0:2, :], in0=rest[:, 0:2, :], in1=one_more[:], op=ALU.add)
-            nc.vector.tensor_scalar_mul(out=rest[:, 2, :], in0=rest[:, 0, :], scalar1=-1.0)
+            ),
+            lambda: nc.vector.tensor_scalar(
+                out=one_more[:],
+                in0=rest[:, 0:2, :],
+                scalar1=math.pi,
+                scalar2=-2.0 * math.pi,
+                op0=ALU.is_gt,
+                op1=ALU.mult,
+            ),
+            lambda: nc.vector.tensor_tensor(out=rest[:, 0:2, :], in0=rest[:, 0:2, :], in1=one_more[:], op=ALU.add),
+            lambda: nc.vector.tensor_scalar_mul(out=rest[:, 2, :], in0=rest[:, 0, :], scalar1=-1.0),
+        ]
 
         def take_stats(first, last):
             for g in range(first, last):
@@ -299,12 +318,14 @@ def tile_mlablock_pa_k_kernel(
         sort_chunk(nc.vector.tensor_copy, *first_and_second(0)[1], pieces=2)
         refill(0)
         for step in range(STEPS):
+            for nth in range(PAIR):
+                grouped = transpose_cached(*first_and_second(step)[nth])
+                if step + 1 < STEPS:
+                    sort_chunk(nc.vector.tensor_copy, *first_and_second(step + 1)[nth])
+                quantise(grouped, *first_and_second(step)[nth])
+                if PAIR * step + nth < len(angle_chain):
+                    angle_chain[PAIR * step + nth]()
             if step + 1 < STEPS:
-                sort_chunk(nc.vector.tensor_copy, *first_and_second(step + 1)[0])
-            for i, c in first_and_second(step):
-                transpose_cached(i, c)
-            if step + 1 < STEPS:
-                sort_chunk(nc.scalar.copy, *first_and_second(step + 1)[1])
                 refill(step + 1)
             if step + PAIR >= STEPS:
                 load_late_words("q", "sorted", SORTED_RING)
@@ -312,9 +333,7 @@ def tile_mlablock_pa_k_kernel(
                 key_passes(step - 1)
             if step == STEPS - 2:
                 take_stats(0, CHUNK_GROUPS)
-            if step == 1:
-                rotary_angles()
-            if step == 3:
+            if PAIR * step == len(angle_chain):
                 nc.scalar.activation(out=trig[:], in_=rest[:], func=ACT.Sin)
         take_stats(CHUNK_GROUPS, GROUPS)
 
@@ -407,7 +426,7 @@ def tile_mlablock_pa_k_kernel(
                     centre(c + 1)
 
         hidden_acc = {}
-        for w in ("q", "k", "v"):
+        for w in ("q", "k"):
             hidden_acc[w] = banks.tile([P, COLS], F32, tag="acc", name="hidden_acc")
         for c in range(CHUNKS):
             for w in ("q", "k"):
@@ -416,10 +435,14 @@ def tile_mlablock_pa_k_kernel(
                 finish_normed(CHUNKS - 1)
                 for i in range(PAIR, LAYERS):
                     store_tile(k_rows, i, rotary(key_raw[i][:]))
-        for c in range(CHUNKS):
-            chunk_passes(hidden_acc["v"], HIDDEN, "v", c)
+        value_halves = [slice(COLS // 2 * half, COLS // 2 * (half + 1)) for half in range(2)]
+        half_acc = [banks.tile([P, COLS // 2], F32, tag="acc", name="half_acc") for half in value_halves]
+        for half, acc in zip(value_halves, half_acc):
+            for g in range(GROUPS):
+                mx_pass(acc, HIDDEN, "v", g, cols=half)
         nc.sync.dma_start(out=q_rows, in_=rotary(hidden_acc["q"][:]))
         store_tile(k_rows, HIDDEN, rotary(hidden_acc["k"][:]))
-        value = stage.tile([P, COLS], F32, tag="value", bufs=3)
-        nc.scalar.copy(out=value[:], in_=hidden_acc["v"][:])
-        store_tile(v_rows, HIDDEN, value[:])
+        for half, acc in zip(value_halves, half_acc):
+            value = stage.tile([P, COLS // 2], F32, tag="value", bufs=3)
+            nc.scalar.copy(out=value[:], in_=acc[:])
+            store_tile(v_rows[:, :, half], HIDDEN, value[:])

@@ -35,8 +35,6 @@ STEPS = CHUNKS * LAYERS // PAIR
 RAW_RING = 12
 SORTED_RING = 4
 AHEAD = RAW_RING // PAIR
-SCALAR_GROUPS = 3
-
 FLOPS = 2 * FEATURES * COLS * (P + 2 * (LAYERS + 1) * P)
 
 
@@ -357,19 +355,14 @@ def tile_mlablock_pa_k_kernel(
 
         def centre(c):
             centred[c] = stage.tile([P, CHUNK_GROUPS, PACK, P], F32, tag="centred", name="centred")
-            nc.scalar.activation(
+            nc.vector.tensor_scalar(
                 out=centred[c][:],
-                in_=hidden_raw[:, CHUNK * c : CHUNK * (c + 1)].rearrange("m (g p t) -> m g t p", g=CHUNK_GROUPS, t=PACK),
-                func=ACT.Identity,
-                scale=rstd[:, 0:1],
-                bias=minus_mean_rstd[:, 0:1],
+                in0=hidden_raw[:, CHUNK * c : CHUNK * (c + 1)].rearrange("m (g p t) -> m g t p", g=CHUNK_GROUPS, t=PACK),
+                scalar1=rstd[:, 0:1],
+                scalar2=minus_mean_rstd[:, 0:1],
+                op0=ALU.mult,
+                op1=ALU.add,
             )
-
-        centre(0)
-        centre(1)
-
-        for i in range(PAIR):
-            store_tile(k_rows, i, rotary(key_raw[i][:]))
 
         gain_bias = const.tile([P, 2 * GROUPS, PACK], F32)
 
@@ -383,6 +376,13 @@ def tile_mlablock_pa_k_kernel(
                 in_=bank[:].bitcast(BF16).rearrange("p u (r e) -> p r u e", e=2)[:, 0 : 2 * GROUPS, :, :],
             )
 
+        spread_gain_bias()
+        centre(0)
+        centre(1)
+
+        for i in range(PAIR):
+            store_tile(k_rows, i, rotary(key_raw[i][:]))
+
         def finish_normed(c):
             planar = stage.tile([P, CHUNK_GROUPS, PACK, P], BF16, align_bytes=64, tag="planar")
             for g in range(CHUNK_GROUPS):
@@ -393,19 +393,9 @@ def tile_mlablock_pa_k_kernel(
                 for t in range(PACK):
                     gain = gain_bias[:, row, t : t + 1]
                     bias = gain_bias[:, GROUPS + row, t : t + 1]
-                    if g < SCALAR_GROUPS:
-                        nc.scalar.activation(
-                            out=planar[:, g, t, :], in_=bank[:, t, :], func=ACT.Identity, scale=gain, bias=bias
-                        )
-                    else:
-                        nc.vector.tensor_scalar(
-                            out=planar[:, g, t, :],
-                            in0=bank[:, t, :],
-                            scalar1=gain,
-                            scalar2=bias,
-                            op0=ALU.mult,
-                            op1=ALU.add,
-                        )
+                    nc.scalar.activation(
+                        out=planar[:, g, t, :], in_=bank[:, t, :], func=ACT.Identity, scale=gain, bias=bias
+                    )
             grouped = stage.tile([P, CHUNK_GROUPS, P, PACK], BF16, align_bytes=64, tag="grouped", bufs=3)
             nc.vector.tensor_copy(out=grouped[:], in_=planar[:].rearrange("p g t m -> p g m t"))
             quantise(grouped, HIDDEN, c)
@@ -418,10 +408,10 @@ def tile_mlablock_pa_k_kernel(
                     value = stage.tile([P, COLS], F32, tag="value", bufs=3)
                     nc.scalar.copy(out=value[:], in_=value_acc[i][:])
                     store_tile(v_rows, i, value[:])
-            if c == 0:
-                spread_gain_bias()
-            else:
+            if c > 0:
                 finish_normed(c - 1)
+                if c == PAIR:
+                    third_key = rotary(key_raw[PAIR][:])
                 if c + 1 < CHUNKS:
                     centre(c + 1)
 
@@ -432,9 +422,9 @@ def tile_mlablock_pa_k_kernel(
             for w in ("q", "k"):
                 chunk_passes(hidden_acc[w], HIDDEN, w, c)
             if c == 0:
+                store_tile(k_rows, PAIR, third_key)
                 finish_normed(CHUNKS - 1)
-                for i in range(PAIR, LAYERS):
-                    store_tile(k_rows, i, rotary(key_raw[i][:]))
+                store_tile(k_rows, PAIR + 1, rotary(key_raw[PAIR + 1][:]))
         value_halves = [slice(COLS // 2 * half, COLS // 2 * (half + 1)) for half in range(2)]
         half_acc = [banks.tile([P, COLS // 2], F32, tag="acc", name="half_acc") for half in value_halves]
         for half, acc in zip(value_halves, half_acc):

@@ -35,6 +35,10 @@ STEPS = CHUNKS * LAYERS // PAIR
 RAW_RING = 12
 SORTED_RING = 4
 AHEAD = RAW_RING // PAIR
+HIDDEN_BEFORE = 2
+GAIN_STEP = 3
+NORMED_RUNS = (11, 14)
+
 FLOPS = 2 * FEATURES * COLS * (P + 2 * (LAYERS + 1) * P)
 
 
@@ -123,18 +127,20 @@ def tile_mlablock_pa_k_kernel(
                         out=cached[(i, c)][:, width * piece : width * (piece + 1)],
                         in_=cache_rows[i, :, CHUNK * c + width * piece : CHUNK * c + width * (piece + 1)],
                     )
-            if (pair == 0) == (c > 0):
+            if pair == LAYERS // PAIR - 1:
                 load_scales("k", c)
                 chunk_words = keep.tile([P, CHUNK_GROUPS, COLS], U32, align_bytes=64, name="words_k%d" % c)
                 load_words("k", chunk_words, CHUNK_GROUPS * c, CHUNK_GROUPS)
-            if step == STEPS - 1:
-                for quarter in range(CHUNKS):
-                    part = slice(CHUNK * quarter, CHUNK * (quarter + 1))
-                    nc.sync.dma_start(out=hidden_raw[:, part], in_=hidden_rows[:, part])
+            if step == 1:
                 nc.sync.dma_start(out=gain_bias_rows[0:GROUPS, :], in_=ln_scale.rearrange("(g k) -> g k", k=GROUP))
                 nc.sync.dma_start(
                     out=gain_bias_rows[GROUPS : 2 * GROUPS, :], in_=ln_bias.rearrange("(g k) -> g k", k=GROUP)
                 )
+
+        def load_hidden():
+            for half in range(2):
+                part = slice(FEATURES // 2 * half, FEATURES // 2 * (half + 1))
+                nc.sync.dma_start(out=hidden_raw[:, part], in_=hidden_rows[:, part])
 
         def load_late_words(w, tag, bufs):
             for j in range(PAIR):
@@ -177,6 +183,18 @@ def tile_mlablock_pa_k_kernel(
                     out=grouped_words[:, 2 * half : 2 * half + 2, :, :], in_=bank[:].rearrange("p g u m -> p g m u")
                 )
             return grouped
+
+        gain_bias = const.tile([P, 2 * GROUPS, PACK], F32)
+
+        def spread_gain_bias():
+            row_words = gain_bias_rows[:].bitcast(F32)
+            bank = banks.tile([P, 2, P], F32, tag="turned")
+            for u in range(2):
+                nc.tensor.transpose(bank[:, u, :], row_words[:, u : GROUP // 2 : 2], identity[:])
+            nc.vector.tensor_copy(
+                out=gain_bias[:].rearrange("p r (u e) -> p r u e", u=2),
+                in_=bank[:].bitcast(BF16).rearrange("p u (r e) -> p r u e", e=2)[:, 0 : 2 * GROUPS, :, :],
+            )
 
         def mx_pass(acc, i, w, g, cols=slice(0, COLS)):
             nc.tensor.matmul_mx(
@@ -239,13 +257,13 @@ def tile_mlablock_pa_k_kernel(
                 load_step(step + AHEAD)
                 return
             c = step + AHEAD - STEPS
+            if c == HIDDEN_BEFORE:
+                load_hidden()
             if c < CHUNKS:
                 load_scales("v", c)
                 load_late_words("v", "raw", RAW_RING)
             else:
-                if c == CHUNKS:
-                    for c_q in range(CHUNKS):
-                        load_scales("q", c_q)
+                load_scales("q", c - CHUNKS)
                 load_late_words("q", "raw", RAW_RING)
 
         partition_index = const.tile([P, 1], I32)
@@ -326,16 +344,17 @@ def tile_mlablock_pa_k_kernel(
             if step + 1 < STEPS:
                 refill(step + 1)
             if step + PAIR >= STEPS:
+                load_scales("q", len(weight_words["q"]) // CHUNK_GROUPS)
                 load_late_words("q", "sorted", SORTED_RING)
             if step >= 1:
                 key_passes(step - 1)
-            if step == STEPS - 2:
-                take_stats(0, CHUNK_GROUPS)
+            if step == GAIN_STEP:
+                spread_gain_bias()
             if PAIR * step == len(angle_chain):
                 nc.scalar.activation(out=trig[:], in_=rest[:], func=ACT.Sin)
-        take_stats(CHUNK_GROUPS, GROUPS)
-
         key_passes(STEPS - 1)
+        store_tile(k_rows, 0, rotary(key_raw[0][:]))
+        take_stats(0, GROUPS)
         nc.scalar.sqrt(out=table_warmer[:], in_=one[:])
 
         mean_var = const.tile([P, 2], F32)
@@ -364,24 +383,10 @@ def tile_mlablock_pa_k_kernel(
                 op1=ALU.add,
             )
 
-        gain_bias = const.tile([P, 2 * GROUPS, PACK], F32)
-
-        def spread_gain_bias():
-            row_words = gain_bias_rows[:].bitcast(F32)
-            bank = banks.tile([P, 2, P], F32, tag="turned")
-            for u in range(2):
-                nc.tensor.transpose(bank[:, u, :], row_words[:, u : GROUP // 2 : 2], identity[:])
-            nc.vector.tensor_copy(
-                out=gain_bias[:].rearrange("p r (u e) -> p r u e", u=2),
-                in_=bank[:].bitcast(BF16).rearrange("p u (r e) -> p r u e", e=2)[:, 0 : 2 * GROUPS, :, :],
-            )
-
-        spread_gain_bias()
         centre(0)
         centre(1)
 
-        for i in range(PAIR):
-            store_tile(k_rows, i, rotary(key_raw[i][:]))
+        store_tile(k_rows, 1, rotary(key_raw[1][:]))
 
         def finish_normed(c):
             planar = stage.tile([P, CHUNK_GROUPS, PACK, P], BF16, align_bytes=64, tag="planar")
@@ -401,19 +406,23 @@ def tile_mlablock_pa_k_kernel(
             quantise(grouped, HIDDEN, c)
 
         value_acc = [banks.tile([P, COLS], F32, tag="acc", name="value_acc") for i in range(LAYERS)]
+        run = 0
         for c in range(CHUNKS):
             for i in range(LAYERS):
                 chunk_passes(value_acc[i], i, "v", c)
+                run += 1
                 if c == CHUNKS - 1:
                     value = stage.tile([P, COLS], F32, tag="value", bufs=3)
                     nc.scalar.copy(out=value[:], in_=value_acc[i][:])
                     store_tile(v_rows, i, value[:])
-            if c > 0:
-                finish_normed(c - 1)
-                if c == PAIR:
-                    third_key = rotary(key_raw[PAIR][:])
-                if c + 1 < CHUNKS:
-                    centre(c + 1)
+                if run in NORMED_RUNS:
+                    n = NORMED_RUNS.index(run)
+                    finish_normed(n)
+                    centre(n + 2)
+                    if n == 0:
+                        third_key = rotary(key_raw[PAIR][:])
+        store_tile(k_rows, PAIR, third_key)
+        finish_normed(2)
 
         hidden_acc = {}
         for w in ("q", "k"):
@@ -422,8 +431,7 @@ def tile_mlablock_pa_k_kernel(
             for w in ("q", "k"):
                 chunk_passes(hidden_acc[w], HIDDEN, w, c)
             if c == 0:
-                store_tile(k_rows, PAIR, third_key)
-                finish_normed(CHUNKS - 1)
+                finish_normed(3)
                 store_tile(k_rows, PAIR + 1, rotary(key_raw[PAIR + 1][:]))
         value_halves = [slice(COLS // 2 * half, COLS // 2 * (half + 1)) for half in range(2)]
         half_acc = [banks.tile([P, COLS // 2], F32, tag="acc", name="half_acc") for half in value_halves]

@@ -35,7 +35,6 @@ STEPS = CHUNKS * LAYERS // PAIR
 RAW_RING = 12
 SORTED_RING = 4
 AHEAD = RAW_RING // PAIR
-HIDDEN_BEFORE = 2
 GAIN_STEP = 3
 NORMED_RUNS = (11, 14)
 
@@ -137,10 +136,9 @@ def tile_mlablock_pa_k_kernel(
                     out=gain_bias_rows[GROUPS : 2 * GROUPS, :], in_=ln_bias.rearrange("(g k) -> g k", k=GROUP)
                 )
 
-        def load_hidden():
-            for half in range(2):
-                part = slice(FEATURES // 2 * half, FEATURES // 2 * (half + 1))
-                nc.sync.dma_start(out=hidden_raw[:, part], in_=hidden_rows[:, part])
+        def load_hidden(half):
+            part = slice(FEATURES // 2 * half, FEATURES // 2 * (half + 1))
+            nc.sync.dma_start(out=hidden_raw[:, part], in_=hidden_rows[:, part])
 
         def load_late_words(w, tag, bufs):
             for j in range(PAIR):
@@ -151,12 +149,12 @@ def tile_mlablock_pa_k_kernel(
         for step in range(AHEAD):
             load_step(step)
 
-        def quantise(grouped, i, c):
-            groups = slice(CHUNK_GROUPS * c, CHUNK_GROUPS * (c + 1))
+        def quantise(grouped, i, first, count):
+            groups = slice(first, first + count)
             nc.vector.quantize_mx(
                 out=codes[i][:, groups, :].rearrange("p g m -> p (g m)").bitcast(FP8X4),
                 scales=code_planes[i][:, groups, :].rearrange("p g m -> p (g m)"),
-                in_=grouped[:].rearrange("p g m t -> p (g m t)"),
+                in_=grouped.rearrange("p g m t -> p (g m t)"),
             )
 
         sorted_words = {}
@@ -257,11 +255,11 @@ def tile_mlablock_pa_k_kernel(
                 load_step(step + AHEAD)
                 return
             c = step + AHEAD - STEPS
-            if c == HIDDEN_BEFORE:
-                load_hidden()
             if c < CHUNKS:
                 load_scales("v", c)
                 load_late_words("v", "raw", RAW_RING)
+                if c < 2:
+                    load_hidden(c)
             else:
                 load_scales("q", c - CHUNKS)
                 load_late_words("q", "raw", RAW_RING)
@@ -338,7 +336,8 @@ def tile_mlablock_pa_k_kernel(
                 grouped = transpose_cached(*first_and_second(step)[nth])
                 if step + 1 < STEPS:
                     sort_chunk(nc.vector.tensor_copy, *first_and_second(step + 1)[nth])
-                quantise(grouped, *first_and_second(step)[nth])
+                i, c = first_and_second(step)[nth]
+                quantise(grouped[:], i, CHUNK_GROUPS * c, CHUNK_GROUPS)
                 if PAIR * step + nth < len(angle_chain):
                     angle_chain[PAIR * step + nth]()
             if step + 1 < STEPS:
@@ -402,8 +401,11 @@ def tile_mlablock_pa_k_kernel(
                         out=planar[:, g, t, :], in_=bank[:, t, :], func=ACT.Identity, scale=gain, bias=bias
                     )
             grouped = stage.tile([P, CHUNK_GROUPS, P, PACK], BF16, align_bytes=64, tag="grouped", bufs=3)
-            nc.vector.tensor_copy(out=grouped[:], in_=planar[:].rearrange("p g t m -> p g m t"))
-            quantise(grouped, HIDDEN, c)
+            count = CHUNK_GROUPS // 2
+            for first in range(0, CHUNK_GROUPS, count):
+                part = slice(first, first + count)
+                nc.vector.tensor_copy(out=grouped[:, part], in_=planar[:, part].rearrange("p g t m -> p g m t"))
+                quantise(grouped[:, part], HIDDEN, CHUNK_GROUPS * c + first, count)
 
         value_acc = [banks.tile([P, COLS], F32, tag="acc", name="value_acc") for i in range(LAYERS)]
         run = 0

@@ -36,7 +36,7 @@ RAW_RING = 12
 SORTED_RING = 4
 AHEAD = RAW_RING // PAIR
 GAIN_STEP = 3
-NORMED_RUNS = (11, 14)
+NORMED_RUNS = (11, 13)
 
 FLOPS = 2 * FEATURES * COLS * (P + 2 * (LAYERS + 1) * P)
 
@@ -255,11 +255,13 @@ def tile_mlablock_pa_k_kernel(
                 load_step(step + AHEAD)
                 return
             c = step + AHEAD - STEPS
+            if c == 0:
+                load_hidden(0)
+            if c == 2:
+                load_hidden(1)
             if c < CHUNKS:
                 load_scales("v", c)
                 load_late_words("v", "raw", RAW_RING)
-                if c < 2:
-                    load_hidden(c)
             else:
                 load_scales("q", c - CHUNKS)
                 load_late_words("q", "raw", RAW_RING)
@@ -352,8 +354,9 @@ def tile_mlablock_pa_k_kernel(
             if PAIR * step == len(angle_chain):
                 nc.scalar.activation(out=trig[:], in_=rest[:], func=ACT.Sin)
         key_passes(STEPS - 1)
+        take_stats(0, GROUPS // 2)
         store_tile(k_rows, 0, rotary(key_raw[0][:]))
-        take_stats(0, GROUPS)
+        take_stats(GROUPS // 2, GROUPS)
         nc.scalar.sqrt(out=table_warmer[:], in_=one[:])
 
         mean_var = const.tile([P, 2], F32)

@@ -35,6 +35,7 @@ STEPS = CHUNKS * LAYERS // PAIR
 RAW_RING = 12
 SORTED_RING = 4
 AHEAD = RAW_RING // PAIR
+HEAD_STEPS = 2
 GAIN_STEP = 3
 NORMED_RUNS = (11, 13)
 
@@ -109,32 +110,42 @@ def tile_mlablock_pa_k_kernel(
 
         def load_words(w, tile_, first_group, groups):
             source = dram_words[w][first_group : first_group + groups].rearrange("g p n t -> p g (n t)")
-            nc.sync.dma_start(out=tile_[:].bitcast(I32), in_=source.bitcast(I32))
+            nc.sync.dma_start(out=tile_.bitcast(I32), in_=source.bitcast(I32))
             for i in range(groups):
                 weight_words[w].append(tile_[:, i, :])
 
         cached = {}
 
+        def load_cached(i, c, features):
+            nc.sync.dma_start(
+                out=cached[(i, c)][:, features],
+                in_=cache_rows[i, :, CHUNK * c + features.start : CHUNK * c + features.stop],
+            )
+
+        def load_first_chunk():
+            for i in range(LAYERS):
+                cached[(i, 0)] = ring.tile([P, CHUNK], BF16, align_bytes=64, tag="raw", name="cached")
+            chunk_words = keep.tile([P, CHUNK_GROUPS, COLS], U32, align_bytes=64, name="words_k0")
+            for half in range(2):
+                for i in range(LAYERS):
+                    load_cached(i, 0, slice(CHUNK // 2 * half, CHUNK // 2 * (half + 1)))
+                if half == 0:
+                    load_scales("k", 0)
+                load_words("k", chunk_words[:, 2 * half : 2 * half + 2, :], 2 * half, 2)
+            nc.sync.dma_start(out=gain_bias_rows[0:GROUPS, :], in_=ln_scale.rearrange("(g k) -> g k", k=GROUP))
+            nc.sync.dma_start(
+                out=gain_bias_rows[GROUPS : 2 * GROUPS, :], in_=ln_bias.rearrange("(g k) -> g k", k=GROUP)
+            )
+
         def load_step(step):
             c, pair = divmod(step, LAYERS // PAIR)
             for i in range(PAIR * pair, PAIR * (pair + 1)):
                 cached[(i, c)] = ring.tile([P, CHUNK], BF16, align_bytes=64, tag="raw", name="cached")
-                pieces = 2 if step == 0 else 1
-                width = CHUNK // pieces
-                for piece in range(pieces):
-                    nc.sync.dma_start(
-                        out=cached[(i, c)][:, width * piece : width * (piece + 1)],
-                        in_=cache_rows[i, :, CHUNK * c + width * piece : CHUNK * c + width * (piece + 1)],
-                    )
+                load_cached(i, c, slice(0, CHUNK))
             if pair == LAYERS // PAIR - 1:
                 load_scales("k", c)
                 chunk_words = keep.tile([P, CHUNK_GROUPS, COLS], U32, align_bytes=64, name="words_k%d" % c)
-                load_words("k", chunk_words, CHUNK_GROUPS * c, CHUNK_GROUPS)
-            if step == 1:
-                nc.sync.dma_start(out=gain_bias_rows[0:GROUPS, :], in_=ln_scale.rearrange("(g k) -> g k", k=GROUP))
-                nc.sync.dma_start(
-                    out=gain_bias_rows[GROUPS : 2 * GROUPS, :], in_=ln_bias.rearrange("(g k) -> g k", k=GROUP)
-                )
+                load_words("k", chunk_words[:], CHUNK_GROUPS * c, CHUNK_GROUPS)
 
         def load_hidden(half):
             part = slice(FEATURES // 2 * half, FEATURES // 2 * (half + 1))
@@ -143,10 +154,11 @@ def tile_mlablock_pa_k_kernel(
         def load_late_words(w, tag, bufs):
             for j in range(PAIR):
                 words = ring.tile([P, 2, COLS], U32, align_bytes=64, tag=tag, bufs=bufs, name="late_words")
-                load_words(w, words, len(weight_words[w]), 2)
+                load_words(w, words[:], len(weight_words[w]), 2)
 
         hidden_raw = keep.tile([P, FEATURES], BF16)
-        for step in range(AHEAD):
+        load_first_chunk()
+        for step in range(HEAD_STEPS, AHEAD):
             load_step(step)
 
         def quantise(grouped, i, first, count):
@@ -157,26 +169,37 @@ def tile_mlablock_pa_k_kernel(
                 in_=grouped.rearrange("p g m t -> p (g m t)"),
             )
 
+        def runs_of(step, nth):
+            if step < HEAD_STEPS:
+                return [(i, 2 * step, 2) for i in range(PAIR * nth, PAIR * (nth + 1))]
+            c, pair = divmod(step, LAYERS // PAIR)
+            return [(PAIR * pair + nth, CHUNK_GROUPS * c, CHUNK_GROUPS)]
+
         sorted_words = {}
 
-        def sort_chunk(copy, i, c, pieces=1):
-            sorted_words[(i, c)] = ring.tile(
+        def sort_words(step, nth):
+            sorted_words[(step, nth)] = ring.tile(
                 [P, CHUNK_GROUPS, 2, P], F32, align_bytes=64, tag="sorted", bufs=SORTED_RING, name="sorted_words"
             )
-            source = cached[(i, c)][:].bitcast(F32).rearrange("m (g p u) -> m g u p", g=CHUNK_GROUPS, u=2)
-            groups = CHUNK_GROUPS // pieces
-            for piece in range(pieces):
-                part = slice(groups * piece, groups * (piece + 1))
-                copy(out=sorted_words[(i, c)][:, part], in_=source[:, part])
+            place = 0
+            for i, first, count in runs_of(step, nth):
+                c, inner = divmod(first, CHUNK_GROUPS)
+                source = cached[(i, c)][:].bitcast(F32).rearrange("m (g p u) -> m g u p", g=CHUNK_GROUPS, u=2)
+                nc.vector.tensor_copy(
+                    out=sorted_words[(step, nth)][:, place : place + count], in_=source[:, inner : inner + count]
+                )
+                place += count
 
-        def transpose_cached(i, c):
+        def transpose_cached(step, nth):
             grouped = stage.tile([P, CHUNK_GROUPS, P, PACK], BF16, align_bytes=64, tag="grouped", bufs=3)
             grouped_words = grouped[:].bitcast(F32)
             for half in range(2):
                 bank = banks.tile([P, 2, 2, P], F32, tag="turned")
                 for g in range(2):
                     for u in range(2):
-                        nc.tensor.transpose(bank[:, g, u, :], sorted_words[(i, c)][:, 2 * half + g, u, :], identity[:])
+                        nc.tensor.transpose(
+                            bank[:, g, u, :], sorted_words[(step, nth)][:, 2 * half + g, u, :], identity[:]
+                        )
                 nc.scalar.copy(
                     out=grouped_words[:, 2 * half : 2 * half + 2, :, :], in_=bank[:].rearrange("p g u m -> p g m u")
                 )
@@ -243,6 +266,11 @@ def tile_mlablock_pa_k_kernel(
         key_raw = {}
 
         def key_passes(step):
+            if step < HEAD_STEPS:
+                for i in range(LAYERS):
+                    for g in range(2 * step, 2 * step + 2):
+                        mx_pass(key_acc[i], i, "k", g)
+                return
             c, pair = divmod(step, LAYERS // PAIR)
             for i in range(PAIR * pair, PAIR * (pair + 1)):
                 chunk_passes(key_acc[i], i, "k", c)
@@ -326,22 +354,21 @@ def tile_mlablock_pa_k_kernel(
             for g in range(first, last):
                 nc.vector.bn_stats(out=stats[:, g, :], in_=hidden_raw[:, GROUP * g : GROUP * (g + 1)])
 
-        def first_and_second(step):
-            c, pair = divmod(step, LAYERS // PAIR)
-            return (PAIR * pair, c), (PAIR * pair + 1, c)
-
-        sort_chunk(nc.vector.tensor_copy, *first_and_second(0)[0], pieces=2)
-        sort_chunk(nc.vector.tensor_copy, *first_and_second(0)[1], pieces=2)
-        refill(0)
+        for nth in range(PAIR):
+            sort_words(0, nth)
         for step in range(STEPS):
             for nth in range(PAIR):
-                grouped = transpose_cached(*first_and_second(step)[nth])
+                grouped = transpose_cached(step, nth)
                 if step + 1 < STEPS:
-                    sort_chunk(nc.vector.tensor_copy, *first_and_second(step + 1)[nth])
-                i, c = first_and_second(step)[nth]
-                quantise(grouped[:], i, CHUNK_GROUPS * c, CHUNK_GROUPS)
+                    sort_words(step + 1, nth)
+                place = 0
+                for i, first, count in runs_of(step, nth):
+                    quantise(grouped[:, place : place + count], i, first, count)
+                    place += count
                 if PAIR * step + nth < len(angle_chain):
                     angle_chain[PAIR * step + nth]()
+            if step == 0:
+                refill(0)
             if step + 1 < STEPS:
                 refill(step + 1)
             if step + PAIR >= STEPS:

import math
from contextlib import ExitStack

import concourse.mybir as mybir
from concourse.masks import make_identity

F32 = mybir.dt.float32
BF16 = mybir.dt.bfloat16
I32 = mybir.dt.int32
U32 = mybir.dt.uint32
U8 = mybir.dt.uint8
FP8X4 = mybir.dt.float8_e4m3fn_x4
ALU = mybir.AluOpType
ACT = mybir.ActivationFunctionType

P = 128
PACK = 4
GROUP = P * PACK
FEATURES = 8192
GROUPS = FEATURES // GROUP
CHUNK_GROUPS = 4
CHUNKS = GROUPS // CHUNK_GROUPS
CHUNK = CHUNK_GROUPS * GROUP
COLS = 512
HEADS = 8
HALF = 32
SEQ = 64
BATCH = 2
LAYERS = 4
HIDDEN = LAYERS
EPS = 1e-5
QUADRANTS = 4
PAIR = 2
STEPS = CHUNKS * LAYERS // PAIR
RAW_RING = 12
SORTED_RING = 4
AHEAD = RAW_RING // PAIR
HEAD_STEPS = 2
GAIN_STEP = 3
NORMED_RUNS = (11, 13)

FLOPS = 2 * FEATURES * COLS * (P + 2 * (LAYERS + 1) * P)


def tile_mlablock_pa_k_kernel(
    tc,
    hidden_states,
    cache_states,
    ln_scale,
    ln_bias,
    Wq_words,
    Wq_scales,
    Wk_words,
    Wk_scales,
    Wv_words,
    Wv_scales,
    out_0,
    out_1,
    out_2,
):
    nc = tc.nc
    with ExitStack() as ctx:
        const = ctx.enter_context(tc.tile_pool(name="const", bufs=1))
        keep = ctx.enter_context(tc.tile_pool(name="keep", bufs=1))
        ring = ctx.enter_context(tc.tile_pool(name="ring", bufs=RAW_RING))
        stage = ctx.enter_context(tc.tile_pool(name="stage", bufs=2))
        banks = ctx.enter_context(tc.psum_pool(name="banks", bufs=4))
        ctx.enter_context(tc.manual_schedule())

        cache_rows = cache_states.rearrange("w b s k -> w (b s) k")
        hidden_rows = hidden_states.rearrange("b s k -> (b s) k")
        q_rows = out_0.rearrange("b s h d -> (b s) (h d)")
        k_rows = out_1.rearrange("b l h d -> b l (h d)")
        v_rows = out_2.rearrange("b l h d -> b l (h d)")
        dram_words = {"q": Wq_words, "k": Wk_words, "v": Wv_words}
        dram_scales = {"q": Wq_scales, "k": Wk_scales, "v": Wv_scales}

        plane_tiles = {}
        for w in ("k", "v", "q"):
            plane_tiles[w] = keep.tile([P, CHUNKS, COLS], U8, align_bytes=64, name="planes_" + w)
        identity = const.tile([P, P], F32)
        make_identity(nc, identity[:])
        for w in ("k", "v", "q"):
            nc.gpsimd.memset(plane_tiles[w][:].bitcast(I32), 0)
        gain_bias_rows = const.tile([P, GROUP], BF16)
        nc.gpsimd.memset(gain_bias_rows[:], 0.0)

        codes = [keep.tile([P, GROUPS, P], U32, align_bytes=64, name="codes%d" % i) for i in range(LAYERS + 1)]
        code_planes = [keep.tile([P, GROUPS, P], U8, align_bytes=64, name="cplanes%d" % i) for i in range(LAYERS + 1)]

        weight_words = {"q": [], "k": [], "v": []}
        weight_planes = {"q": [], "k": [], "v": []}

        one = const.tile([P, 1], F32)
        nc.vector.memset(one[:], 1.0)
        table_warmer = const.tile([P, 1], F32)
        nc.scalar.activation(out=table_warmer[:], in_=one[:], func=ACT.Sin)

        def load_scales(w, c):
            for quadrant in range(QUADRANTS):
                first = 32 * quadrant
                nc.sync.dma_start(
                    out=plane_tiles[w][first : first + 16, c, :].bitcast(I32),
                    in_=dram_scales[w][
                        CHUNK_GROUPS * c : CHUNK_GROUPS * (c + 1), 4 * quadrant : 4 * quadrant + 4, :
                    ].bitcast(I32),
                )
            for i in range(CHUNK_GROUPS):
                weight_planes[w].append(plane_tiles[w][4 * i : P, c, :])

        def load_words(w, tile_, first_group, groups):
            source = dram_words[w][first_group : first_group + groups].rearrange("g p n t -> p g (n t)")
            nc.sync.dma_start(out=tile_.bitcast(I32), in_=source.bitcast(I32))
            for i in range(groups):
                weight_words[w].append(tile_[:, i, :])

        cached = {}

        def load_cached(i, c, features):
            nc.sync.dma_start(
                out=cached[(i, c)][:, features],
                in_=cache_rows[i, :, CHUNK * c + features.start : CHUNK * c + features.stop],
            )

        def load_first_chunk():
            for i in range(LAYERS):
                cached[(i, 0)] = ring.tile([P, CHUNK], BF16, align_bytes=64, tag="raw", name="cached")
            chunk_words = keep.tile([P, CHUNK_GROUPS, COLS], U32, align_bytes=64, name="words_k0")
            for half in range(2):
                for i in range(LAYERS):
                    load_cached(i, 0, slice(CHUNK // 2 * half, CHUNK // 2 * (half + 1)))
                if half == 0:
                    load_scales("k", 0)
                load_words("k", chunk_words[:, 2 * half : 2 * half + 2, :], 2 * half, 2)
            nc.sync.dma_start(out=gain_bias_rows[0:GROUPS, :], in_=ln_scale.rearrange("(g k) -> g k", k=GROUP))
            nc.sync.dma_start(
                out=gain_bias_rows[GROUPS : 2 * GROUPS, :], in_=ln_bias.rearrange("(g k) -> g k", k=GROUP)
            )

        def load_step(step):
            c, pair = divmod(step, LAYERS // PAIR)
            for i in range(PAIR * pair, PAIR * (pair + 1)):
                cached[(i, c)] = ring.tile([P, CHUNK], BF16, align_bytes=64, tag="raw", name="cached")
                load_cached(i, c, slice(0, CHUNK))
            if pair == LAYERS // PAIR - 1:
                load_scales("k", c)
                chunk_words = keep.tile([P, CHUNK_GROUPS, COLS], U32, align_bytes=64, name="words_k%d" % c)
                load_words("k", chunk_words[:], CHUNK_GROUPS * c, CHUNK_GROUPS)

        def load_hidden(half):
            part = slice(FEATURES // 2 * half, FEATURES // 2 * (half + 1))
            nc.sync.dma_start(out=hidden_raw[:, part], in_=hidden_rows[:, part])

        def load_late_words(w, tag, bufs):
            for j in range(PAIR):
                words = ring.tile([P, 2, COLS], U32, align_bytes=64, tag=tag, bufs=bufs, name="late_words")
                load_words(w, words[:], len(weight_words[w]), 2)

        hidden_raw = keep.tile([P, FEATURES], BF16)
        load_first_chunk()
        for step in range(HEAD_STEPS, AHEAD):
            load_step(step)

        def quantise(grouped, i, first, count):
            groups = slice(first, first + count)
            nc.vector.quantize_mx(
                out=codes[i][:, groups, :].rearrange("p g m -> p (g m)").bitcast(FP8X4),
                scales=code_planes[i][:, groups, :].rearrange("p g m -> p (g m)"),
                in_=grouped.rearrange("p g m t -> p (g m t)"),
            )

        def runs_of(step, nth):
            if step < HEAD_STEPS:
                return [(i, 2 * step, 2) for i in range(PAIR * nth, PAIR * (nth + 1))]
            c, pair = divmod(step, LAYERS // PAIR)
            return [(PAIR * pair + nth, CHUNK_GROUPS * c, CHUNK_GROUPS)]

        sorted_words = {}

        def sort_words(step, nth):
            sorted_words[(step, nth)] = ring.tile(
                [P, CHUNK_GROUPS, 2, P], F32, align_bytes=64, tag="sorted", bufs=SORTED_RING, name="sorted_words"
            )
            place = 0
            for i, first, count in runs_of(step, nth):
                c, inner = divmod(first, CHUNK_GROUPS)
                source = cached[(i, c)][:].bitcast(F32).rearrange("m (g p u) -> m g u p", g=CHUNK_GROUPS, u=2)
                nc.vector.tensor_copy(
                    out=sorted_words[(step, nth)][:, place : place + count], in_=source[:, inner : inner + count]
                )
                place += count

        def transpose_cached(step, nth):
            grouped = stage.tile([P, CHUNK_GROUPS, P, PACK], BF16, align_bytes=64, tag="grouped", bufs=3)
            grouped_words = grouped[:].bitcast(F32)
            for half in range(2):
                bank = banks.tile([P, 2, 2, P], F32, tag="turned")
                for g in range(2):
                    for u in range(2):
                        nc.tensor.transpose(
                            bank[:, g, u, :], sorted_words[(step, nth)][:, 2 * half + g, u, :], identity[:]
                        )
                nc.scalar.copy(
                    out=grouped_words[:, 2 * half : 2 * half + 2, :, :], in_=bank[:].rearrange("p g u m -> p g m u")
                )
            return grouped

        gain_bias = const.tile([P, 2 * GROUPS, PACK], F32)

        def spread_gain_bias():
            row_words = gain_bias_rows[:].bitcast(F32)
            bank = banks.tile([P, 2, P], F32, tag="turned")
            for u in range(2):
                nc.tensor.transpose(bank[:, u, :], row_words[:, u : GROUP // 2 : 2], identity[:])
            nc.vector.tensor_copy(
                out=gain_bias[:].rearrange("p r (u e) -> p r u e", u=2),
                in_=bank[:].bitcast(BF16).rearrange("p u (r e) -> p r u e", e=2)[:, 0 : 2 * GROUPS, :, :],
            )

        def mx_pass(acc, i, w, g, cols=slice(0, COLS)):
            nc.tensor.matmul_mx(
                out=acc[:],
                lhsT=codes[i][:, g, :].bitcast(FP8X4),
                lhsT_scale=code_planes[i][:, g, :],
                rhs=weight_words[w][g][:, cols].bitcast(FP8X4),
                rhs_scale=weight_planes[w][g][:, cols],
                start=(g == 0),
                stop=(g == GROUPS - 1),
            )

        def chunk_passes(acc, i, w, c):
            for g in range(CHUNK_GROUPS * c, CHUNK_GROUPS * (c + 1)):
                mx_pass(acc, i, w, g)

        def store_tile(rows, i, result):
            for b in range(BATCH):
                nc.sync.dma_start(out=rows[b, SEQ * i : SEQ * (i + 1), :], in_=result[SEQ * b : SEQ * (b + 1), :])

        def rotary(source):
            x = source.rearrange("p (h two i) -> p h two i", two=2, i=HALF)
            direct = stage.tile([P, HEADS, 2, HALF], F32, tag="direct", bufs=3)
            crossed = stage.tile([P, HEADS, 2, HALF], F32, tag="crossed")
            nc.vector.tensor_tensor(
                out=direct[:].rearrange("p h two i -> p (h two) i"),
                in0=source.rearrange("p (j i) -> p j i", i=HALF),
                in1=cos.unsqueeze(1).to_broadcast([P, 2 * HEADS, HALF]),
                op=ALU.mult,
            )
            nc.vector.tensor_tensor(
                out=crossed[:, :, 0, :],
                in0=x[:, :, 1, :],
                in1=minus_sin.unsqueeze(1).to_broadcast([P, HEADS, HALF]),
                op=ALU.mult,
            )
            nc.vector.tensor_tensor(
                out=crossed[:, :, 1, :],
                in0=x[:, :, 0, :],
                in1=sin.unsqueeze(1).to_broadcast([P, HEADS, HALF]),
                op=ALU.mult,
            )
            nc.vector.tensor_tensor(out=direct[:], in0=direct[:], in1=crossed[:], op=ALU.add)
            return direct[:].rearrange("p h two i -> p (h two i)")

        stats = const.tile([P, GROUPS, 6], F32)
        key_acc = [banks.tile([P, COLS], F32, tag="acc", name="key_acc") for i in range(LAYERS)]
        key_raw = {}

        def key_passes(step):
            if step < HEAD_STEPS:
                for i in range(LAYERS):
                    for g in range(2 * step, 2 * step + 2):
                        mx_pass(key_acc[i], i, "k", g)
                return
            c, pair = divmod(step, LAYERS // PAIR)
            for i in range(PAIR * pair, PAIR * (pair + 1)):
                chunk_passes(key_acc[i], i, "k", c)
                if c == CHUNKS - 1:
                    key_raw[i] = stage.tile([P, COLS], F32, tag="key_raw", bufs=LAYERS, name="key_raw")
                    nc.scalar.copy(out=key_raw[i][:], in_=key_acc[i][:])

        def refill(step):
            if step + AHEAD < STEPS:
                load_step(step + AHEAD)
                return
            c = step + AHEAD - STEPS
            if c == 0:
                load_hidden(0)
            if c == 2:
                load_hidden(1)
            if c < CHUNKS:
                load_scales("v", c)
                load_late_words("v", "raw", RAW_RING)
            else:
                load_scales("q", c - CHUNKS)
                load_late_words("q", "raw", RAW_RING)

        partition_index = const.tile([P, 1], I32)
        pos_int = const.tile([P, 1], I32)
        pos = const.tile([P, 1], F32)
        freq = const.tile([P, HALF], F32)
        angle = const.tile([P, 2, HALF], F32)
        turns_int = const.tile([P, 2, HALF], I32)
        turns = const.tile([P, 2, HALF], F32)
        rest = const.tile([P, 3, HALF], F32)
        one_more = const.tile([P, 2, HALF], F32)
        trig = const.tile([P, 3, HALF], F32)
        sin = trig[:, 0, :]
        cos = trig[:, 1, :]
        minus_sin = trig[:, 2, :]

        nc.gpsimd.iota(partition_index[:], pattern=[[0, 1]], base=0, channel_multiplier=1)
        nc.vector.memset(freq[:, 0:1], 1.0)

        def double_freq(n):
            nc.vector.tensor_scalar_mul(out=freq[:, n : 2 * n], in0=freq[:, 0:n], scalar1=10000.0 ** (-n / HALF))

        def take_angles():
            nc.vector.tensor_scalar(out=angle[:, 0, :], in0=freq[:], scalar1=pos[:, 0:1], scalar2=None, op0=ALU.mult)
            nc.vector.tensor_scalar(
                out=angle[:, 1, :], in0=freq[:], scalar1=pos[:, 0:1], scalar2=math.pi / 2, op0=ALU.mult, op1=ALU.add
            )

        angle_chain = [
            lambda: nc.vector.tensor_single_scalar(
                out=pos_int[:], in_=partition_index[:], scalar=SEQ - 1, op=ALU.bitwise_and
            ),
            lambda: nc.vector.tensor_copy(out=pos[:], in_=pos_int[:]),
            lambda: double_freq(1),
            lambda: double_freq(2),
            lambda: double_freq(4),
            lambda: double_freq(8),
            lambda: double_freq(16),
            take_angles,
            lambda: nc.vector.tensor_scalar(
                out=turns_int[:], in0=angle[:], scalar1=0.5 / math.pi, scalar2=None, op0=ALU.mult
            ),
            lambda: nc.vector.tensor_copy(out=turns[:], in_=turns_int[:]),
            lambda: nc.vector.scalar_tensor_tensor(
                out=rest[:, 0:2, :], in0=turns[:], scalar=-2.0 * math.pi, in1=angle[:], op0=ALU.mult, op1=ALU.add
            ),
            lambda: nc.vector.tensor_scalar(
                out=one_more[:],
                in0=rest[:, 0:2, :],
                scalar1=math.pi,
                scalar2=-2.0 * math.pi,
                op0=ALU.is_gt,
                op1=ALU.mult,
            ),
            lambda: nc.vector.tensor_tensor(out=rest[:, 0:2, :], in0=rest[:, 0:2, :], in1=one_more[:], op=ALU.add),
            lambda: nc.vector.tensor_scalar_mul(out=rest[:, 2, :], in0=rest[:, 0, :], scalar1=-1.0),
        ]

        def take_stats(first, last):
            for g in range(first, last):
                nc.vector.bn_stats(out=stats[:, g, :], in_=hidden_raw[:, GROUP * g : GROUP * (g + 1)])

        for nth in range(PAIR):
            sort_words(0, nth)
        for step in range(STEPS):
            for nth in range(PAIR):
                grouped = transpose_cached(step, nth)
                if step + 1 < STEPS:
                    sort_words(step + 1, nth)
                place = 0
                for i, first, count in runs_of(step, nth):
                    quantise(grouped[:, place : place + count], i, first, count)
                    place += count
                if PAIR * step + nth < len(angle_chain):
                    angle_chain[PAIR * step + nth]()
            if step == 0:
                refill(0)
            if step + 1 < STEPS:
                refill(step + 1)
            if step + PAIR >= STEPS:
                load_scales("q", len(weight_words["q"]) // CHUNK_GROUPS)
                load_late_words("q", "sorted", SORTED_RING)
            if step >= 1:
                key_passes(step - 1)
            if step == GAIN_STEP:
                spread_gain_bias()
            if PAIR * step == len(angle_chain):
                nc.scalar.activation(out=trig[:], in_=rest[:], func=ACT.Sin)
        key_passes(STEPS - 1)
        take_stats(0, GROUPS // 2)
        store_tile(k_rows, 0, rotary(key_raw[0][:]))
        take_stats(GROUPS // 2, GROUPS)
        nc.scalar.sqrt(out=table_warmer[:], in_=one[:])

        mean_var = const.tile([P, 2], F32)
        nc.vector.bn_aggr(out=mean_var[:], in_=stats[:].rearrange("p g s -> p (g s)"))
        var_eps = const.tile([P, 1], F32)
        nc.vector.tensor_scalar_add(out=var_eps[:], in0=mean_var[:, 1:2], scalar1=EPS)
        std = const.tile([P, 1], F32)
        nc.scalar.sqrt(out=std[:], in_=var_eps[:])
        rstd = const.tile([P, 1], F32)
        nc.vector.reciprocal(out=rstd[:], in_=std[:])
        minus_mean_rstd = const.tile([P, 1], F32)
        nc.vector.scalar_tensor_tensor(
            out=minus_mean_rstd[:], in0=mean_var[:, 0:1], scalar=-1.0, in1=rstd[:], op0=ALU.mult, op1=ALU.mult
        )

        centred = {}

        def centre(c):
            centred[c] = stage.tile([P, CHUNK_GROUPS, PACK, P], F32, tag="centred", name="centred")
            nc.vector.tensor_scalar(
                out=centred[c][:],
                in0=hidden_raw[:, CHUNK * c : CHUNK * (c + 1)].rearrange("m (g p t) -> m g t p", g=CHUNK_GROUPS, t=PACK),
                scalar1=rstd[:, 0:1],
                scalar2=minus_mean_rstd[:, 0:1],
                op0=ALU.mult,
                op1=ALU.add,
            )

        centre(0)
        centre(1)

        store_tile(k_rows, 1, rotary(key_raw[1][:]))

        def finish_normed(c):
            planar = stage.tile([P, CHUNK_GROUPS, PACK, P], BF16, align_bytes=64, tag="planar")
            for g in range(CHUNK_GROUPS):
                bank = banks.tile([P, PACK, P], F32, tag="turned")
                for t in range(PACK):
                    nc.tensor.transpose(bank[:, t, :], centred[c][:, g, t, :], identity[:])
                row = CHUNK_GROUPS * c + g
                for t in range(PACK):
                    gain = gain_bias[:, row, t : t + 1]
                    bias = gain_bias[:, GROUPS + row, t : t + 1]
                    nc.scalar.activation(
                        out=planar[:, g, t, :], in_=bank[:, t, :], func=ACT.Identity, scale=gain, bias=bias
                    )
            grouped = stage.tile([P, CHUNK_GROUPS, P, PACK], BF16, align_bytes=64, tag="grouped", bufs=3)
            count = CHUNK_GROUPS // 2
            for first in range(0, CHUNK_GROUPS, count):
                part = slice(first, first + count)
                nc.vector.tensor_copy(out=grouped[:, part], in_=planar[:, part].rearrange("p g t m -> p g m t"))
                quantise(grouped[:, part], HIDDEN, CHUNK_GROUPS * c + first, count)

        value_acc = [banks.tile([P, COLS], F32, tag="acc", name="value_acc") for i in range(LAYERS)]
        run = 0
        for c in range(CHUNKS):
            for i in range(LAYERS):
                chunk_passes(value_acc[i], i, "v", c)
                run += 1
                if c == CHUNKS - 1:
                    value = stage.tile([P, COLS], F32, tag="value", bufs=3)
                    nc.scalar.copy(out=value[:], in_=value_acc[i][:])
                    store_tile(v_rows, i, value[:])
                if run in NORMED_RUNS:
                    n = NORMED_RUNS.index(run)
                    finish_normed(n)
                    centre(n + 2)
                    if n == 0:
                        third_key = rotary(key_raw[PAIR][:])
        store_tile(k_rows, PAIR, third_key)
        finish_normed(2)

        hidden_acc = {}
        for w in ("q", "k"):
            hidden_acc[w] = banks.tile([P, COLS], F32, tag="acc", name="hidden_acc")
        for c in range(CHUNKS):
            for w in ("q", "k"):
                chunk_passes(hidden_acc[w], HIDDEN, w, c)
            if c == 0:
                finish_normed(3)
                store_tile(k_rows, PAIR + 1, rotary(key_raw[PAIR + 1][:]))
        value_halves = [slice(COLS // 2 * half, COLS // 2 * (half + 1)) for half in range(2)]
        half_acc = [banks.tile([P, COLS // 2], F32, tag="acc", name="half_acc") for half in value_halves]
        for half, acc in zip(value_halves, half_acc):
            for g in range(GROUPS):
                mx_pass(acc, HIDDEN, "v", g, cols=half)
        nc.sync.dma_start(out=q_rows, in_=rotary(hidden_acc["q"][:]))
        store_tile(k_rows, HIDDEN, rotary(hidden_acc["k"][:]))
        for half, acc in zip(value_halves, half_acc):
            value = stage.tile([P, COLS // 2], F32, tag="value", bufs=3)
            nc.scalar.copy(out=value[:], in_=acc[:])
            store_tile(v_rows[:, :, half], HIDDEN, value[:])
